import numpy as np
import ml_dtypes


def mxq(x, axis, fmt="e4m3"):
    dtype, down = {"e4m3": (ml_dtypes.float8_e4m3fn, 7), "e5m2": (ml_dtypes.float8_e5m2, 14)}[fmt]
    v = np.moveaxis(np.asarray(x, np.float32).astype(ml_dtypes.bfloat16).astype(np.float64), axis, -1)
    blocks = v.reshape(v.shape[:-1] + (-1, 32))
    amax = np.abs(blocks).max(-1, keepdims=True)
    byte = np.maximum(np.where(amax > 0, np.frexp(amax)[1] - 1 + 127, 0) - down, 1)
    scale = np.exp2(byte - 127.0)
    codes = (blocks / scale).astype(np.float32).astype(dtype).astype(np.float64)
    return np.moveaxis((codes * scale).reshape(v.shape), -1, axis)


WIDE = False


def mx_kscale(k):
    if not WIDE:
        return np.ones(k)
    levels = np.array([10, -10, 5, -5, 0])
    if k % 512:
        return np.exp2(np.random.permutation(np.resize(levels, k // 32))).repeat(32)
    a = np.empty((k // 512, 16))
    for p in range(k // 512):
        a[p, :8] = np.random.permutation(np.resize(levels, 8))
        for g in range(8):
            far = levels[np.abs(levels - a[p, g]) >= 10]
            a[p, g + 8] = far[np.random.randint(len(far))]
    return np.exp2(a.ravel()).repeat(32)


BF16 = ml_dtypes.bfloat16


def bf(x):
    return np.asarray(x, np.float32).astype(BF16)


def f64(x):
    return np.asarray(x).astype(np.float64)


B, IN, H = 2048, 512, 512
G = 4 * H
EPS = 1e-5


def _layernorm(v, gamma, beta):
    mean = np.mean(v, axis=-1, keepdims=True)
    var = np.mean(np.square(v - mean), axis=-1, keepdims=True)
    return (v - mean) / np.sqrt(var + EPS) * gamma + beta


def sigmoid(v):
    return 1.0 / (1.0 + np.exp(-v))


def draw0():
    s, t = mx_kscale(IN), mx_kscale(H)
    return {
        "x": bf(np.random.standard_normal((B, IN)) * s),
        "h_prev": bf(np.random.standard_normal((B, H)) * t),
        "c_prev": bf(np.random.standard_normal((B, H))),
        "W_ih": bf(np.random.standard_normal((IN, G)) / np.sqrt(IN) / s[:, None]),
        "W_hh": bf(np.random.standard_normal((H, G)) / np.sqrt(H) / t[:, None]),
        "gamma_ih": bf(1.0 + 0.2 * np.random.standard_normal(G)),
        "beta_ih": bf(0.3 * np.random.standard_normal(G)),
        "gamma_hh": bf(1.0 + 0.2 * np.random.standard_normal(G)),
        "beta_hh": bf(0.3 * np.random.standard_normal(G)),
        "gamma_c": bf(1.0 + 0.2 * np.random.standard_normal(H)),
        "beta_c": bf(0.3 * np.random.standard_normal(H)),
    }


def core(x, h_prev, c_prev, W_ih, W_hh, gamma_ih, beta_ih, gamma_hh, beta_hh, gamma_c, beta_c):
    a_ih = mxq(f64(x), 1, "e4m3") @ mxq(f64(W_ih), 0, "e4m3")
    a_hh = mxq(f64(h_prev), 1, "e4m3") @ mxq(f64(W_hh), 0, "e4m3")
    gates_ih = _layernorm(a_ih, f64(gamma_ih), f64(beta_ih))
    gates_hh = _layernorm(a_hh, f64(gamma_hh), f64(beta_hh))
    gates = gates_ih + gates_hh
    i_g, f_g, g_g, o_g = np.split(gates, 4, axis=1)
    i_t = sigmoid(i_g)
    f_t = sigmoid(f_g)
    g_t = np.tanh(g_g)
    o_t = sigmoid(o_g)
    c_t = f_t * f64(c_prev) + i_t * g_t
    h_t = o_t * np.tanh(_layernorm(c_t, f64(gamma_c), f64(beta_c)))
    return (h_t, c_t)


def e4m3fn_bytes(y):
    return np.clip(np.asarray(y, np.float64), -448.0, 448.0).astype(np.float32).astype(ml_dtypes.float8_e4m3fn).view(np.uint8)


def e4m3fn_values(b):
    return np.asarray(b, np.uint8).view(ml_dtypes.float8_e4m3fn).astype(np.float64)


def setup_inputs():
    d = draw0()
    x0 = np.asarray(d['x']).astype(np.float64)
    s = (np.max(np.abs(x0), axis=(0,), keepdims=True) / 448.0).astype(np.float32)
    out = {}
    for k, v in d.items():
        if k == 'x':
            out['x_bytes'] = e4m3fn_bytes(x0 / s.astype(np.float64))
            out['x_scale'] = s
        else:
            out[k] = v
    return out


def reference(x_bytes, x_scale, h_prev, c_prev, W_ih, W_hh, gamma_ih, beta_ih, gamma_hh, beta_hh, gamma_c, beta_c):
    return core(e4m3fn_values(x_bytes) * x_scale.astype(np.float64), h_prev, c_prev, W_ih, W_hh, gamma_ih, beta_ih, gamma_hh, beta_hh, gamma_c, beta_c)

@@ -1,0 +1,500 @@
+from contextlib import ExitStack
+
+import concourse.mybir as mybir
+from concourse.masks import make_identity
+
+F32 = mybir.dt.float32
+BF16 = mybir.dt.bfloat16
+U32 = mybir.dt.uint32
+U8 = mybir.dt.uint8
+FP8 = mybir.dt.float8_e4m3fn
+FP8X4 = mybir.dt.float8_e4m3fn_x4
+ALU = mybir.AluOpType
+ACT = mybir.ActivationFunctionType
+
+TOKENS, K, H, GATES = 2048, 512, 512, 2048
+EPS = 1e-5
+FLOPS = 2 * 2 * TOKENS * K * GATES
+
+P = 128
+PACK = 4
+BANK = 512
+TILES = TOKENS // P
+PAIRS = TILES // 2
+PIECES = 8 * TILES
+GROUPS = GATES // P
+UNITS = GROUPS * PAIRS
+STATS_DIM = 6
+GATE_ORDER = (0, 2, 1, 3)
+I_GATE, G_GATE, F_GATE, O_GATE = 0, 1, 2, 3
+
+NORM_LAG = 18
+TURN_LAG = NORM_LAG + 6
+CELL_LAG = TURN_LAG + 16
+CELL_F_C, CELL_C, CELL_STATS, CELL_AGGR, CELL_AFFINE, CELL_TANH, CELL_H = 2, 6, 7, 8, 10, 14, 16
+IG_SLOTS = (11, 15)
+PREP_QUANT, PREP_WIDEN, PREP_COPY = 1, 3, 4
+W_HH_QUANT_SLOTS = (2, 5, 9, 7)
+W_HH_COPY_SLOT_VECTOR = 2
+W_HH_COPY_SLOT_SCALAR = 4
+GAIN_TURN_SLOT, GAIN_COPY_SLOT = 8, 10
+CELL_GAIN_SPREAD_SLOTS, CELL_GAIN_COPY_SLOTS = (12, 15), (13, 16)
+VECTOR_SHIFT_FROM_UNIT = UNITS - TURN_LAG
+VECTOR_AFFINE_FROM_TILE = TILES - 3
+LAST_SLOT = CELL_LAG + 8 * (TILES - 1) + CELL_H
+
+
+def tile_layernormlstmcell_kernel(
+    tc,
+    x_bytes,
+    x_scale,
+    h_prev,
+    c_prev,
+    W_ih,
+    W_hh,
+    gamma_ih,
+    beta_ih,
+    gamma_hh,
+    beta_hh,
+    gamma_c,
+    beta_c,
+    out_0,
+    out_1,
+):
+    nc = tc.nc
+    with ExitStack() as ctx:
+        const = ctx.enter_context(tc.tile_pool(name="const", bufs=1))
+        wstage = ctx.enter_context(tc.tile_pool(name="wstage", bufs=4))
+        prep = ctx.enter_context(tc.tile_pool(name="prep", bufs=2))
+        ypool = ctx.enter_context(tc.tile_pool(name="ypool", bufs=12))
+        gates = ctx.enter_context(tc.tile_pool(name="gates", bufs=2))
+        cell = ctx.enter_context(tc.tile_pool(name="cell", bufs=3))
+        small = ctx.enter_context(tc.tile_pool(name="small", bufs=3))
+        ps_stat = ctx.enter_context(tc.psum_pool(name="ps_stat", bufs=2))
+        ps_norm = ctx.enter_context(tc.psum_pool(name="ps_norm", bufs=2))
+        ps_unit = ctx.enter_context(tc.psum_pool(name="ps_unit", bufs=2))
+        ps_one = ctx.enter_context(tc.psum_pool(name="ps_one", bufs=1))
+        ctx.enter_context(tc.manual_schedule())
+
+        w_views = (
+            W_ih.rearrange("(p j) w -> p j w", j=PACK),
+            W_hh.rearrange("(p j) w -> p j w", j=PACK),
+        )
+        w_raw = {}
+
+        def load_w(m, q_lo, q_hi):
+            t = wstage.tile([P, PACK, (q_hi - q_lo) * BANK], BF16, name="w_raw", tag="w_raw", bufs=5)
+            nc.sync.dma_start(out=t[:], in_=w_views[m][:, :, q_lo * BANK:q_hi * BANK])
+            for q in range(q_lo, q_hi):
+                w_raw[(m, q)] = t[:, :, (q - q_lo) * BANK:(q - q_lo + 1) * BANK]
+
+        x_sb = const.tile([P, TILES, K], U8, name="x_sb", tag="x_sb")
+        h_sb = const.tile([P, TILES, K], BF16, name="h_sb", tag="h_sb")
+        c_sb = const.tile([P, TILES, H], BF16, name="c_sb", tag="c_sb")
+        x_view = x_bytes.rearrange("(n p) k -> p n k", p=P)
+        h_view = h_prev.rearrange("(n p) k -> p n k", p=P)
+        c_view = c_prev.rearrange("(n p) k -> p n k", p=P)
+
+        def load_acts(lo, hi):
+            nc.sync.dma_start(out=x_sb[:, lo:hi, :], in_=x_view[:, lo:hi, :])
+            nc.sync.dma_start(out=h_sb[:, lo:hi, :], in_=h_view[:, lo:hi, :])
+
+        scale_row = const.tile([P, K], F32, name="scale_row", tag="scale_row")
+        cell_gain_row = const.tile([P, 2 * H], BF16, name="cell_gain_row", tag="cell_gain_row")
+        gain_rows = const.tile([P, P], BF16, name="gain_rows", tag="gain_rows")
+
+        load_w(0, 0, 1)
+        nc.gpsimd.memset(scale_row[:], 0.0)
+        nc.sync.dma_start(out=scale_row[0:1, :], in_=x_scale)
+        load_acts(0, 2)
+        load_w(0, 1, 2)
+        load_w(0, 2, 4)
+        load_acts(2, 4)
+        load_w(1, 0, 2)
+        load_w(1, 2, 4)
+        nc.vector.memset(gain_rows[:], 0.0)
+        for i, vec in enumerate((gamma_ih, gamma_hh, beta_ih, beta_hh)):
+            nc.sync.dma_start(out=gain_rows[GROUPS * i:GROUPS * (i + 1), :], in_=vec.rearrange("(j p) -> j p", p=P))
+        nc.gpsimd.memset(cell_gain_row[:], 0.0)
+        nc.sync.dma_start(out=cell_gain_row[0:1, 0:H], in_=gamma_c.rearrange("(o k) -> o k", o=1))
+        nc.sync.dma_start(out=cell_gain_row[0:1, H:2 * H], in_=beta_c.rearrange("(o k) -> o k", o=1))
+        for lo in (4, 8, 12):
+            load_acts(lo, lo + 4)
+        for lo in (0, 4, 8, 12):
+            nc.sync.dma_start(out=c_sb[:, lo:lo + 4, :], in_=c_view[:, lo:lo + 4, :])
+
+        ones_f32 = const.tile([P, P], F32, name="ones_f32", tag="ones_f32")
+        nc.gpsimd.memset(ones_f32[:], 1.0)
+        warm = const.tile([P, 1], F32, name="warm", tag="warm")
+        nc.gpsimd.memset(warm[:], 0.0)
+        nc.scalar.activation(out=warm[:], in_=warm[:], func=ACT.Sigmoid)
+        ident = const.tile([P, P], F32, name="ident", tag="ident")
+        make_identity(nc, ident[:])
+        ident_bf16 = const.tile([P, P], BF16, name="ident_bf16", tag="ident_bf16")
+        make_identity(nc, ident_bf16[:])
+        ones_bf16 = const.tile([P, P], BF16, name="ones_bf16", tag="ones_bf16")
+        nc.gpsimd.memset(ones_bf16[:], 1.0)
+        neg_half = const.tile([P, 1], F32, name="neg_half", tag="neg_half")
+        nc.gpsimd.memset(neg_half[:], -0.5)
+        scale_all = const.tile([P, K], F32, name="scale_all", tag="scale_all")
+        gamma_c_all = const.tile([P, H], BF16, name="gamma_c_all", tag="gamma_c_all")
+        beta_c_all = const.tile([P, H], BF16, name="beta_c_all", tag="beta_c_all")
+        gain_cols = const.tile([P, 4 * GROUPS], F32, name="gain_cols", tag="gain_cols")
+        beta_cols = const.tile([P, GROUPS], F32, name="beta_cols", tag="beta_cols")
+
+        w_codes = []
+        w_scales = []
+        for m in range(2):
+            codes = const.tile([P, GATES], U32, name="w_codes%d" % m, tag="w_codes%d" % m, align_bytes=64)
+            scales = const.tile([P, GATES], U8, name="w_scales%d" % m, tag="w_scales%d" % m, align_bytes=64)
+            w_codes.append(codes)
+            w_scales.append(scales)
+        w_grouped = {}
+
+        def w_interleave(m, q, copy):
+            t = wstage.tile([P, BANK, PACK], BF16, name="w_grouped", tag="w_grouped", align_bytes=64)
+            copy(out=t[:], in_=w_raw[(m, q)].rearrange("p j w -> p w j"))
+            w_grouped[(m, q)] = t
+
+        def w_quantize(m, q):
+            cols = slice(q * BANK, (q + 1) * BANK)
+            nc.vector.quantize_mx(
+                out=w_codes[m][:, cols].bitcast(FP8X4),
+                scales=w_scales[m][:, cols],
+                in_=w_grouped[(m, q)][:].rearrange("p w j -> p (w j)"),
+            )
+
+        x_bf16 = {}
+        turned = {}
+        a_grouped = {}
+        a_codes = {}
+        a_scales = {}
+
+        def a_widen(n):
+            t = prep.tile([P, K], BF16, name="x_bf16", tag="x_bf16", bufs=3)
+            nc.vector.tensor_tensor(out=t[:], in0=x_sb[:, n, :].bitcast(FP8), in1=scale_all[:], op=ALU.mult)
+            x_bf16[n] = t
+
+        def a_turn(n, m):
+            if m == 0:
+                t = ps_one.tile([P, 2 * 2, P], F32, name="late", tag="late")
+                turned[n] = t
+            words = (x_bf16[n][:] if m == 0 else h_sb[:, n, :]).bitcast(F32)
+            for u in range(2):
+                nc.tensor.transpose(turned[n][:, 2 * m + u, :], words[:, u:K // 2:2], ident[:])
+
+        def a_copy(n):
+            t = prep.tile([P, 2 * P * PACK], BF16, name="a_grouped", tag="a_grouped", align_bytes=64)
+            nc.scalar.copy(
+                out=t[:].bitcast(F32).rearrange("p (m r u) -> p m r u", m=2, u=2),
+                in_=turned[n][:].rearrange("p (m u) r -> p m r u", u=2),
+            )
+            a_grouped[n] = t
+
+        def a_quantize(n):
+            codes = prep.tile([P, 2 * P], U32, name="a_codes", tag="a_codes", bufs=8, align_bytes=64)
+            scales = prep.tile([P, 2 * P], U8, name="a_scales", tag="a_scales", bufs=8, align_bytes=64)
+            nc.vector.quantize_mx(out=codes[:].bitcast(FP8X4), scales=scales[:], in_=a_grouped[n][:])
+            a_codes[n] = codes
+            a_scales[n] = scales
+
+        def product_piece(pool, tag, n, m, q):
+            tokens = slice(m * P, (m + 1) * P)
+            cols = slice(q * BANK, (q + 1) * BANK)
+            acc = pool.tile([P, BANK], F32, name=tag, tag=tag)
+            nc.tensor.matmul_mx(
+                out=acc[:],
+                lhsT=a_codes[n][:, tokens].bitcast(FP8X4),
+                lhsT_scale=a_scales[n][:, tokens],
+                rhs=w_codes[m][:, cols].bitcast(FP8X4),
+                rhs_scale=w_scales[m][:, cols],
+                start=True,
+                stop=True,
+            )
+            return acc
+
+        def norm_factors(mean_var, with_shift, tag, bufs):
+            t = small.tile([P, 4], F32, name=tag, tag=tag, bufs=bufs)
+            nc.gpsimd.tensor_scalar(
+                out=t[:, 0:1], in0=mean_var[:, 1:2], scalar1=1.0, scalar2=EPS, op0=ALU.mult, op1=ALU.add
+            )
+            nc.gpsimd.tensor_tensor(out=t[:, 1:2], in0=t[:, 0:1], in1=neg_half[:], op=ALU.pow)
+            if with_shift:
+                nc.gpsimd.tensor_scalar(
+                    out=t[:, 2:3], in0=mean_var[:, 0:1], scalar1=t[:, 1:2], scalar2=-1.0, op0=ALU.mult, op1=ALU.mult
+                )
+            return t
+
+        scale_ps = ps_one.tile([P, K], F32, name="early", tag="early")
+        nc.tensor.matmul(out=scale_ps[:], lhsT=ones_f32[:], rhs=scale_row[:], start=True, stop=True)
+        nc.scalar.copy(out=scale_all[:], in_=scale_ps[:])
+        w_interleave(0, 0, nc.vector.tensor_copy)
+        a_widen(0)
+        w_interleave(0, 1, nc.scalar.copy)
+        a_turn(0, 0)
+        a_turn(0, 1)
+        a_widen(1)
+        w_quantize(0, 0)
+        w_interleave(0, 2, nc.vector.tensor_copy)
+        a_copy(0)
+        w_interleave(0, 3, nc.scalar.copy)
+        w_quantize(0, 1)
+        a_turn(1, 0)
+        a_turn(1, 1)
+        a_quantize(0)
+        w_quantize(0, 2)
+        a_copy(1)
+        a_widen(2)
+        w_quantize(0, 3)
+        a_quantize(1)
+        w_interleave(1, 0, nc.scalar.copy)
+        w_interleave(1, 1, nc.scalar.copy)
+
+        stat_acc = {}
+        norm_acc = {}
+        stats = {}
+        factors = {}
+        y = {}
+        unit_ps = {}
+        shifted = {}
+        gate = {}
+        spread_ps = {}
+        back_ps = {}
+        f_c = {}
+        c_new = {}
+        c_stats = {}
+        c_mean_var = {}
+        c_factors = {}
+        c_normed = {}
+
+        def stat_piece(e):
+            pair, w = divmod(e, 16)
+            m, v = divmod(w, 8)
+            r, q = divmod(v, 4)
+            return 2 * pair + r, m, q
+
+        def norm_piece(i):
+            pair, w = divmod(i, 16)
+            g, v = divmod(w, 4)
+            r, m = divmod(v, 2)
+            return pair, g, r, m
+
+        def unit_place(u):
+            pair, w = divmod(u, GROUPS)
+            g, jj = divmod(w, 4)
+            return pair, g, jj, 4 * GATE_ORDER[g] + jj
+
+        def half_gate(pair, g, half):
+            return gate[(pair, g)][:, 2 * half:2 * half + 2, :].rearrange("p j t -> p (j t)")
+
+        def vector_slot(t):
+            u = t - TURN_LAG - 2
+            if 0 <= u < UNITS:
+                pair, g, jj, j = unit_place(u)
+                if jj == 0:
+                    tl = gates.tile([P, 4, 2 * P], F32, name="gate%d" % g, tag="gate%d" % g)
+                    gate[(pair, g)] = tl
+                nc.vector.scalar_tensor_tensor(
+                    out=gate[(pair, g)][:, jj, :],
+                    in0=unit_ps[u][:, 1, :, :].rearrange("p r t -> p (r t)"),
+                    scalar=gain_cols[:, GROUPS + j:GROUPS + j + 1],
+                    in1=shifted[u][:],
+                    op0=ALU.mult,
+                    op1=ALU.add,
+                )
+            u = t - TURN_LAG - 1
+            if VECTOR_SHIFT_FROM_UNIT <= u < UNITS:
+                j = unit_place(u)[3]
+                tl = prep.tile([P, 2 * P], F32, name="shifted", tag="shifted", bufs=3)
+                nc.vector.tensor_scalar(
+                    out=tl[:],
+                    in0=unit_ps[u][:, 0, :, :].rearrange("p r t -> p (r t)"),
+                    scalar1=gain_cols[:, j:j + 1],
+                    scalar2=beta_cols[:, j:j + 1],
+                    op0=ALU.mult,
+                    op1=ALU.add,
+                )
+                shifted[u] = tl
+            e = t - 1
+            if 0 <= e < PIECES:
+                if e % 4 == 0:
+                    tl = small.tile([P, 4, STATS_DIM], F32, name="stats", tag="stats")
+                    stats[e // 4] = tl
+                nc.vector.bn_stats(out=stats[e // 4][:, e % 4, :], in_=stat_acc[e][:])
+            e = t - 2
+            if 0 <= e < PIECES and e % 4 == 3:
+                mean_var = small.tile([P, 2], F32, name="mean_var", tag="mean_var")
+                nc.vector.bn_aggr(out=mean_var[:], in_=stats[e // 4][:].rearrange("p q s -> p (q s)"))
+                factors[stat_piece(e)[0:2]] = norm_factors(mean_var, True, "factors", 10)
+            first, step = divmod(t - CELL_LAG, 8)
+            for n, step in ((first, step), (first - 1, step + 8), (first - 2, step + 16)):
+                if not 0 <= n < TILES:
+                    continue
+                rows = slice(n * P, (n + 1) * P)
+                if step == CELL_F_C:
+                    tl = cell.tile([P, H], F32, name="f_c", tag="f_c", bufs=2)
+                    nc.vector.tensor_tensor(out=tl[:], in0=back_ps[("f", n)][:], in1=c_sb[:, n, :], op=ALU.mult)
+                    f_c[n] = tl
+                elif step == CELL_C:
+                    tl = cell.tile([P, H], F32, name="c_new", tag="c_new")
+                    nc.vector.tensor_tensor(out=tl[:], in0=back_ps[("ig", n)][:], in1=f_c[n][:], op=ALU.add)
+                    nc.sync.dma_start(out=out_1[rows, :], in_=tl[:])
+                    c_new[n] = tl
+                elif step == CELL_STATS:
+                    tl = small.tile([P, STATS_DIM], F32, name="c_stats", tag="c_stats")
+                    nc.vector.bn_stats(out=tl[:], in_=c_new[n][:])
+                    c_stats[n] = tl
+                elif step == CELL_AGGR:
+                    mean_var = small.tile([P, 2], F32, name="c_mean_var", tag="c_mean_var")
+                    nc.vector.bn_aggr(out=mean_var[:], in_=c_stats[n][:])
+                    on_gpsimd = n < VECTOR_AFFINE_FROM_TILE
+                    c_factors[n] = norm_factors(mean_var, on_gpsimd, "c_factors", 3)
+                    tl = cell.tile([P, H], F32, name="c_normed", tag="c_normed")
+                    if on_gpsimd:
+                        nc.gpsimd.tensor_scalar(
+                            out=tl[:],
+                            in0=c_new[n][:],
+                            scalar1=c_factors[n][:, 1:2],
+                            scalar2=c_factors[n][:, 2:3],
+                            op0=ALU.mult,
+                            op1=ALU.add,
+                        )
+                    else:
+                        nc.vector.scalar_tensor_tensor(
+                            out=tl[:],
+                            in0=c_new[n][:],
+                            scalar=mean_var[:, 0:1],
+                            in1=gamma_c_all[:],
+                            op0=ALU.subtract,
+                            op1=ALU.mult,
+                        )
+                    c_normed[n] = tl
+                elif step == CELL_AFFINE:
+                    v = c_normed[n][:]
+                    if n < VECTOR_AFFINE_FROM_TILE:
+                        nc.gpsimd.tensor_tensor(out=v, in0=v, in1=gamma_c_all[:], op=ALU.mult)
+                        nc.gpsimd.tensor_tensor(out=v, in0=v, in1=beta_c_all[:], op=ALU.add)
+                    else:
+                        nc.vector.scalar_tensor_tensor(
+                            out=v, in0=v, scalar=c_factors[n][:, 1:2], in1=beta_c_all[:], op0=ALU.mult, op1=ALU.add
+                        )
+                elif step == CELL_H:
+                    tl = cell.tile([P, H], F32, name="h_new", tag="h_new")
+                    nc.vector.tensor_tensor(out=tl[:], in0=back_ps[("o", n)][:], in1=c_normed[n][:], op=ALU.mult)
+                    nc.sync.dma_start(out=out_0[rows, :], in_=tl[:])
+            pair, step = divmod(t - TURN_LAG, 16)
+            if 0 <= pair < PAIRS and step in IG_SLOTS:
+                half = IG_SLOTS.index(step)
+                iv = half_gate(pair, I_GATE, half)
+                nc.gpsimd.tensor_tensor(out=iv, in0=iv, in1=half_gate(pair, G_GATE, half), op=ALU.mult)
+            if t == W_HH_COPY_SLOT_VECTOR:
+                w_interleave(1, 3, nc.vector.tensor_copy)
+            if t in W_HH_QUANT_SLOTS:
+                w_quantize(1, W_HH_QUANT_SLOTS.index(t))
+            period, place = divmod(t, 8)
+            if place == PREP_WIDEN and period + 3 < TILES:
+                a_widen(period + 3)
+            if place == PREP_QUANT and 2 <= period + 1 < TILES:
+                a_quantize(period + 1)
+
+        def scalar_slot(t):
+            u = t - TURN_LAG - 1
+            if 0 <= u < VECTOR_SHIFT_FROM_UNIT:
+                j = unit_place(u)[3]
+                tl = prep.tile([P, 2 * P], F32, name="shifted", tag="shifted", bufs=3)
+                nc.scalar.activation(
+                    out=tl[:],
+                    in_=unit_ps[u][:, 0, :, :].rearrange("p r t -> p (r t)"),
+                    func=ACT.Identity,
+                    bias=beta_cols[:, j:j + 1],
+                    scale=gain_cols[:, j:j + 1],
+                )
+                shifted[u] = tl
+            i = t - NORM_LAG - 1
+            if 0 <= i < PIECES:
+                pair, g, r, m = norm_piece(i)
+                fac = factors[(2 * pair + r, m)]
+                tl = ypool.tile([P, BANK], F32, name="y", tag="y")
+                nc.scalar.activation(
+                    out=tl[:], in_=norm_acc[i][:], func=ACT.Identity, bias=fac[:, 2:3], scale=fac[:, 1:2]
+                )
+                y[(pair, g, r, m)] = tl
+            pair, step = divmod(t - TURN_LAG - 3, 16)
+            if 0 <= pair < PAIRS and step % 2 == 0:
+                g, half = divmod(step // 2, 2)
+                v = half_gate(pair, g, half)
+                nc.scalar.activation(out=v, in_=v, func=(ACT.Tanh if g == G_GATE else ACT.Sigmoid))
+            n, step = divmod(t - CELL_LAG - CELL_TANH, 8)
+            if step == 0 and 0 <= n < TILES:
+                nc.scalar.activation(out=c_normed[n][:], in_=c_normed[n][:], func=ACT.Tanh)
+            period, place = divmod(t, 8)
+            if place == PREP_COPY and period + 2 < TILES:
+                a_copy(period + 2)
+            if t == W_HH_COPY_SLOT_SCALAR:
+                w_interleave(1, 2, nc.scalar.copy)
+            if t == GAIN_COPY_SLOT:
+                nc.scalar.copy(out=gain_cols[:], in_=spread_ps["gains"][:, 0:4 * GROUPS])
+                nc.gpsimd.tensor_tensor(
+                    out=beta_cols[:],
+                    in0=gain_cols[:, 2 * GROUPS:3 * GROUPS],
+                    in1=gain_cols[:, 3 * GROUPS:4 * GROUPS],
+                    op=ALU.add,
+                )
+            elif t in CELL_GAIN_COPY_SLOTS:
+                which = CELL_GAIN_COPY_SLOTS.index(t)
+                nc.scalar.copy(out=(gamma_c_all, beta_c_all)[which][:], in_=spread_ps[which][:])
+
+        def turn_back(what, n, g, tag, half):
+            if half == 0:
+                tl = ps_one.tile([P, H], F32, name=tag, tag=tag)
+                back_ps[(what, n)] = tl
+            for jj in (2 * half, 2 * half + 1):
+                nc.tensor.transpose(
+                    back_ps[(what, n)][:, jj * P:(jj + 1) * P],
+                    gate[(n // 2, g)][:, jj, (n % 2) * P:(n % 2 + 1) * P],
+                    ident[:],
+                )
+
+        def tensor_slot(t):
+            if t == GAIN_TURN_SLOT:
+                tl = ps_one.tile([P, P], BF16, name="early", tag="early")
+                nc.tensor.transpose(tl[:], gain_rows[:], ident_bf16[:])
+                spread_ps["gains"] = tl
+            elif t in CELL_GAIN_SPREAD_SLOTS:
+                which = CELL_GAIN_SPREAD_SLOTS.index(t)
+                tl = ps_one.tile([P, H], F32, name="early", tag="early")
+                nc.tensor.matmul(
+                    out=tl[:], lhsT=ones_bf16[:], rhs=cell_gain_row[:, which * H:(which + 1) * H], start=True, stop=True
+                )
+                spread_ps[which] = tl
+            period, place = divmod(t, 8)
+            n = (t - place - CELL_LAG) // 8
+            half = place % 2
+            if place in (0, 1) and 0 <= n < TILES:
+                turn_back("f", n, F_GATE, "early", half)
+            elif place in (2, 3) and period + 2 < TILES:
+                a_turn(period + 2, half)
+            elif place in (4, 5) and 0 <= n < TILES:
+                turn_back("ig", n, I_GATE, "early", half)
+            elif place in (6, 7) and 0 <= n - 1 < TILES:
+                turn_back("o", n - 1, O_GATE, "late", half)
+            if t < PIECES:
+                n, m, q = stat_piece(t)
+                stat_acc[t] = product_piece(ps_stat, "stat_acc", n, m, q)
+            i = t - NORM_LAG
+            if 0 <= i < PIECES:
+                pair, g, r, m = norm_piece(i)
+                norm_acc[i] = product_piece(ps_norm, "norm_acc", 2 * pair + r, m, GATE_ORDER[g])
+            u = t - TURN_LAG
+            if 0 <= u < UNITS:
+                pair, g, jj, j = unit_place(u)
+                tl = ps_unit.tile([P, 2, 2, P], F32, name="unit_ps", tag="unit_ps")
+                for m in range(2):
+                    for r in range(2):
+                        nc.tensor.transpose(tl[:, m, r, :], y[(pair, g, r, m)][:, jj * P:(jj + 1) * P], ident[:])
+                unit_ps[u] = tl
+
+        for t in range(LAST_SLOT + 1):
+            vector_slot(t)
+            scalar_slot(t)
+            tensor_slot(t)

@@ -31,17 +31,33 @@ I_GATE, G_GATE, F_GATE, O_GATE = 0, 1, 2, 3
 NORM_LAG = 18
 TURN_LAG = NORM_LAG + 6
 CELL_LAG = TURN_LAG + 16
-CELL_F_C, CELL_C, CELL_STATS, CELL_AGGR, CELL_AFFINE, CELL_TANH, CELL_H = 2, 6, 7, 8, 10, 14, 16
+F_TURN, F_C, IG_TURN, C_SUM, C_STATS, C_AGGR, C_AFFINE, C_TANH, O_TURN, H_OUT = 0, 1, 2, 3, 4, 5, 6, 7, 8, 9
+CELL_STEPS = (0, 2, 4, 6, 7, 8, 10, 14, 14, 16)
+LAST_CELL_STEPS = (0, 2, 2, 4, 5, 6, 8, 9, 4, 11)
+LAST_CELL_LEAD = 2
 IG_SLOTS = (11, 15)
 PREP_QUANT, PREP_WIDEN, PREP_COPY = 1, 3, 4
-W_HH_QUANT_SLOTS = (2, 5, 9, 7)
+W_HH_QUANT_SLOTS = (4, 6, 9, 10)
 W_HH_COPY_SLOT_VECTOR = 2
 W_HH_COPY_SLOT_SCALAR = 4
 GAIN_TURN_SLOT, GAIN_COPY_SLOT = 8, 10
 CELL_GAIN_SPREAD_SLOTS, CELL_GAIN_COPY_SLOTS = (12, 15), (13, 16)
 VECTOR_SHIFT_FROM_UNIT = UNITS - TURN_LAG
+VECTOR_SHIFT_TO_UNIT = UNITS - (TURN_LAG - NORM_LAG)
 VECTOR_AFFINE_FROM_TILE = TILES - 3
-LAST_SLOT = CELL_LAG + 8 * (TILES - 1) + CELL_H
+
+
+def cell_start(n):
+    if n < TILES - 2:
+        return CELL_LAG + 8 * n
+    return CELL_LAG + 8 * (TILES - 2) - LAST_CELL_LEAD
+
+
+def cell_slot(n, step):
+    return cell_start(n) + (CELL_STEPS if n < TILES - 2 else LAST_CELL_STEPS)[step]
+
+
+LAST_SLOT = CELL_LAG + 8 * (TILES - 2) - LAST_CELL_LEAD + LAST_CELL_STEPS[H_OUT]
 
 
 def tile_layernormlstmcell_kernel(
@@ -156,6 +172,9 @@ def tile_layernormlstmcell_kernel(
             copy(out=t[:], in_=w_raw[(m, q)].rearrange("p j w -> p w j"))
             w_grouped[(m, q)] = t
 
+        def gpsimd_copy(out, in_):
+            nc.gpsimd.tensor_scalar(out=out, in0=in_, scalar1=1.0, scalar2=0.0, op0=ALU.mult, op1=ALU.add)
+
         def w_quantize(m, q):
             cols = slice(q * BANK, (q + 1) * BANK)
             nc.vector.quantize_mx(
@@ -235,7 +254,7 @@ def tile_layernormlstmcell_kernel(
         a_turn(0, 1)
         a_widen(1)
         w_quantize(0, 0)
-        w_interleave(0, 2, nc.vector.tensor_copy)
+        w_interleave(0, 2, gpsimd_copy)
         a_copy(0)
         w_interleave(0, 3, nc.scalar.copy)
         w_quantize(0, 1)
@@ -247,7 +266,7 @@ def tile_layernormlstmcell_kernel(
         a_widen(2)
         w_quantize(0, 3)
         a_quantize(1)
-        w_interleave(1, 0, nc.scalar.copy)
+        w_interleave(1, 0, gpsimd_copy)
         w_interleave(1, 1, nc.scalar.copy)
 
         stat_acc = {}
@@ -303,7 +322,7 @@ def tile_layernormlstmcell_kernel(
                     op1=ALU.add,
                 )
             u = t - TURN_LAG - 1
-            if VECTOR_SHIFT_FROM_UNIT <= u < UNITS:
+            if VECTOR_SHIFT_FROM_UNIT <= u < VECTOR_SHIFT_TO_UNIT:
                 j = unit_place(u)[3]
                 tl = prep.tile([P, 2 * P], F32, name="shifted", tag="shifted", bufs=3)
                 nc.vector.tensor_scalar(
@@ -326,25 +345,22 @@ def tile_layernormlstmcell_kernel(
                 mean_var = small.tile([P, 2], F32, name="mean_var", tag="mean_var")
                 nc.vector.bn_aggr(out=mean_var[:], in_=stats[e // 4][:].rearrange("p q s -> p (q s)"))
                 factors[stat_piece(e)[0:2]] = norm_factors(mean_var, True, "factors", 10)
-            first, step = divmod(t - CELL_LAG, 8)
-            for n, step in ((first, step), (first - 1, step + 8), (first - 2, step + 16)):
-                if not 0 <= n < TILES:
-                    continue
+            for n in sorted(range(TILES), key=lambda i: (-cell_start(i), i)):
                 rows = slice(n * P, (n + 1) * P)
-                if step == CELL_F_C:
+                if t == cell_slot(n, F_C):
                     tl = cell.tile([P, H], F32, name="f_c", tag="f_c", bufs=2)
                     nc.vector.tensor_tensor(out=tl[:], in0=back_ps[("f", n)][:], in1=c_sb[:, n, :], op=ALU.mult)
                     f_c[n] = tl
-                elif step == CELL_C:
+                elif t == cell_slot(n, C_SUM):
                     tl = cell.tile([P, H], F32, name="c_new", tag="c_new")
                     nc.vector.tensor_tensor(out=tl[:], in0=back_ps[("ig", n)][:], in1=f_c[n][:], op=ALU.add)
                     nc.sync.dma_start(out=out_1[rows, :], in_=tl[:])
                     c_new[n] = tl
-                elif step == CELL_STATS:
+                elif t == cell_slot(n, C_STATS):
                     tl = small.tile([P, STATS_DIM], F32, name="c_stats", tag="c_stats")
                     nc.vector.bn_stats(out=tl[:], in_=c_new[n][:])
                     c_stats[n] = tl
-                elif step == CELL_AGGR:
+                elif t == cell_slot(n, C_AGGR):
                     mean_var = small.tile([P, 2], F32, name="c_mean_var", tag="c_mean_var")
                     nc.vector.bn_aggr(out=mean_var[:], in_=c_stats[n][:])
                     on_gpsimd = n < VECTOR_AFFINE_FROM_TILE
@@ -369,7 +385,7 @@ def tile_layernormlstmcell_kernel(
                             op1=ALU.mult,
                         )
                     c_normed[n] = tl
-                elif step == CELL_AFFINE:
+                elif t == cell_slot(n, C_AFFINE):
                     v = c_normed[n][:]
                     if n < VECTOR_AFFINE_FROM_TILE:
                         nc.gpsimd.tensor_tensor(out=v, in0=v, in1=gamma_c_all[:], op=ALU.mult)
@@ -378,7 +394,7 @@ def tile_layernormlstmcell_kernel(
                         nc.vector.scalar_tensor_tensor(
                             out=v, in0=v, scalar=c_factors[n][:, 1:2], in1=beta_c_all[:], op0=ALU.mult, op1=ALU.add
                         )
-                elif step == CELL_H:
+                elif t == cell_slot(n, H_OUT):
                     tl = cell.tile([P, H], F32, name="h_new", tag="h_new")
                     nc.vector.tensor_tensor(out=tl[:], in0=back_ps[("o", n)][:], in1=c_normed[n][:], op=ALU.mult)
                     nc.sync.dma_start(out=out_0[rows, :], in_=tl[:])
@@ -388,7 +404,7 @@ def tile_layernormlstmcell_kernel(
                 iv = half_gate(pair, I_GATE, half)
                 nc.gpsimd.tensor_tensor(out=iv, in0=iv, in1=half_gate(pair, G_GATE, half), op=ALU.mult)
             if t == W_HH_COPY_SLOT_VECTOR:
-                w_interleave(1, 3, nc.vector.tensor_copy)
+                w_interleave(1, 3, gpsimd_copy)
             if t in W_HH_QUANT_SLOTS:
                 w_quantize(1, W_HH_QUANT_SLOTS.index(t))
             period, place = divmod(t, 8)
@@ -399,7 +415,7 @@ def tile_layernormlstmcell_kernel(
 
         def scalar_slot(t):
             u = t - TURN_LAG - 1
-            if 0 <= u < VECTOR_SHIFT_FROM_UNIT:
+            if 0 <= u < VECTOR_SHIFT_FROM_UNIT or VECTOR_SHIFT_TO_UNIT <= u < UNITS:
                 j = unit_place(u)[3]
                 tl = prep.tile([P, 2 * P], F32, name="shifted", tag="shifted", bufs=3)
                 nc.scalar.activation(
@@ -424,9 +440,9 @@ def tile_layernormlstmcell_kernel(
                 g, half = divmod(step // 2, 2)
                 v = half_gate(pair, g, half)
                 nc.scalar.activation(out=v, in_=v, func=(ACT.Tanh if g == G_GATE else ACT.Sigmoid))
-            n, step = divmod(t - CELL_LAG - CELL_TANH, 8)
-            if step == 0 and 0 <= n < TILES:
-                nc.scalar.activation(out=c_normed[n][:], in_=c_normed[n][:], func=ACT.Tanh)
+            for n in range(TILES):
+                if t == cell_slot(n, C_TANH):
+                    nc.scalar.activation(out=c_normed[n][:], in_=c_normed[n][:], func=ACT.Tanh)
             period, place = divmod(t, 8)
             if place == PREP_COPY and period + 2 < TILES:
                 a_copy(period + 2)
@@ -444,9 +460,13 @@ def tile_layernormlstmcell_kernel(
                 which = CELL_GAIN_COPY_SLOTS.index(t)
                 nc.scalar.copy(out=(gamma_c_all, beta_c_all)[which][:], in_=spread_ps[which][:])
 
-        def turn_back(what, n, g, tag, half):
+        def turn_back(what, n, g, half):
             if half == 0:
-                tl = ps_one.tile([P, H], F32, name=tag, tag=tag)
+                if n >= TILES - 2:
+                    pool, tag = (ps_norm, "norm_acc") if what == "ig" else (ps_stat, "stat_acc")
+                else:
+                    pool, tag = ps_one, ("late" if what == "o" else "early")
+                tl = pool.tile([P, H], F32, name=tag, tag=tag)
                 back_ps[(what, n)] = tl
             for jj in (2 * half, 2 * half + 1):
                 nc.tensor.transpose(
@@ -467,17 +487,13 @@ def tile_layernormlstmcell_kernel(
                     out=tl[:], lhsT=ones_bf16[:], rhs=cell_gain_row[:, which * H:(which + 1) * H], start=True, stop=True
                 )
                 spread_ps[which] = tl
+            for n in range(TILES):
+                for what, g, step in (("f", F_GATE, F_TURN), ("ig", I_GATE, IG_TURN), ("o", O_GATE, O_TURN)):
+                    if t - cell_slot(n, step) in (0, 1):
+                        turn_back(what, n, g, t - cell_slot(n, step))
             period, place = divmod(t, 8)
-            n = (t - place - CELL_LAG) // 8
-            half = place % 2
-            if place in (0, 1) and 0 <= n < TILES:
-                turn_back("f", n, F_GATE, "early", half)
-            elif place in (2, 3) and period + 2 < TILES:
-                a_turn(period + 2, half)
-            elif place in (4, 5) and 0 <= n < TILES:
-                turn_back("ig", n, I_GATE, "early", half)
-            elif place in (6, 7) and 0 <= n - 1 < TILES:
-                turn_back("o", n - 1, O_GATE, "late", half)
+            if place in (2, 3) and period + 2 < TILES:
+                a_turn(period + 2, place % 2)
             if t < PIECES:
                 n, m, q = stat_piece(t)
                 stat_acc[t] = product_piece(ps_stat, "stat_acc", n, m, q)

@@ -37,7 +37,7 @@ LAST_CELL_STEPS = (0, 2, 2, 4, 5, 6, 8, 9, 4, 11)
 LAST_CELL_LEAD = 2
 IG_SLOTS = (11, 15)
 PREP_QUANT, PREP_WIDEN, PREP_COPY = 1, 3, 4
-W_HH_QUANT_SLOTS = (4, 6, 9, 10)
+W_HH_QUANT_SLOTS = (2, 5, 9, 7)
 W_HH_COPY_SLOT_VECTOR = 2
 W_HH_COPY_SLOT_SCALAR = 4
 GAIN_TURN_SLOT, GAIN_COPY_SLOT = 8, 10
@@ -172,9 +172,6 @@ def tile_layernormlstmcell_kernel(
             copy(out=t[:], in_=w_raw[(m, q)].rearrange("p j w -> p w j"))
             w_grouped[(m, q)] = t
 
-        def gpsimd_copy(out, in_):
-            nc.gpsimd.tensor_scalar(out=out, in0=in_, scalar1=1.0, scalar2=0.0, op0=ALU.mult, op1=ALU.add)
-
         def w_quantize(m, q):
             cols = slice(q * BANK, (q + 1) * BANK)
             nc.vector.quantize_mx(
@@ -254,7 +251,7 @@ def tile_layernormlstmcell_kernel(
         a_turn(0, 1)
         a_widen(1)
         w_quantize(0, 0)
-        w_interleave(0, 2, gpsimd_copy)
+        w_interleave(0, 2, nc.vector.tensor_copy)
         a_copy(0)
         w_interleave(0, 3, nc.scalar.copy)
         w_quantize(0, 1)
@@ -266,7 +263,7 @@ def tile_layernormlstmcell_kernel(
         a_widen(2)
         w_quantize(0, 3)
         a_quantize(1)
-        w_interleave(1, 0, gpsimd_copy)
+        w_interleave(1, 0, nc.scalar.copy)
         w_interleave(1, 1, nc.scalar.copy)
 
         stat_acc = {}
@@ -404,7 +401,7 @@ def tile_layernormlstmcell_kernel(
                 iv = half_gate(pair, I_GATE, half)
                 nc.gpsimd.tensor_tensor(out=iv, in0=iv, in1=half_gate(pair, G_GATE, half), op=ALU.mult)
             if t == W_HH_COPY_SLOT_VECTOR:
-                w_interleave(1, 3, gpsimd_copy)
+                w_interleave(1, 3, nc.vector.tensor_copy)
             if t in W_HH_QUANT_SLOTS:
                 w_quantize(1, W_HH_QUANT_SLOTS.index(t))
             period, place = divmod(t, 8)

@@ -169,7 +169,10 @@ def tile_layernormlstmcell_kernel(
 
         def w_interleave(m, q, copy):
             t = wstage.tile([P, BANK, PACK], BF16, name="w_grouped", tag="w_grouped", align_bytes=64)
-            copy(out=t[:], in_=w_raw[(m, q)].rearrange("p j w -> p w j"))
+            copy(
+                out=t[:].rearrange("p (c i) j -> p c j i", i=4),
+                in_=w_raw[(m, q)].rearrange("p j (c i) -> p c j i", i=4),
+            )
             w_grouped[(m, q)] = t
 
         def w_quantize(m, q):

@@ -19,6 +19,7 @@ FLOPS = 2 * 2 * TOKENS * K * GATES
 P = 128
 PACK = 4
 BANK = 512
+CHUNK_BYTES = PACK * BANK * 2
 TILES = TOKENS // P
 PAIRS = TILES // 2
 PIECES = 8 * TILES
@@ -28,23 +29,23 @@ STATS_DIM = 6
 GATE_ORDER = (0, 2, 1, 3)
 I_GATE, G_GATE, F_GATE, O_GATE = 0, 1, 2, 3
 
-NORM_LAG = 18
-TURN_LAG = NORM_LAG + 6
-CELL_LAG = TURN_LAG + 16
-F_TURN, F_C, IG_TURN, C_SUM, C_STATS, C_AGGR, C_AFFINE, C_TANH, O_TURN, H_OUT = 0, 1, 2, 3, 4, 5, 6, 7, 8, 9
-CELL_STEPS = (0, 2, 4, 6, 7, 8, 10, 14, 14, 16)
-LAST_CELL_STEPS = (0, 2, 2, 4, 5, 6, 8, 9, 4, 11)
-LAST_CELL_LEAD = 2
-IG_SLOTS = (11, 15)
-PREP_QUANT, PREP_WIDEN, PREP_COPY = 1, 3, 4
+NORM_LAG = 11
+TURN_LAG = NORM_LAG + 11
+CELL_LAG = TURN_LAG + 13
+F_TURN, F_C, IG_TURN, C_SUM, C_SQUARE, C_GAIN, C_SHIFT, C_TANH, O_TURN, H_OUT = 0, 1, 2, 3, 4, 5, 6, 7, 8, 9
+CELL_STEPS = (0, 2, 4, 6, 7, 9, 12, 14, 14, 16)
+LAST_CELL_STEPS = (0, 2, 2, 4, 6, 6, 9, 10, 4, 12)
+LAST_CELL_LEAD = 0
+IG_SLOTS = (8, 13)
+PREP_WIDEN, PREP_TURN, PREP_COPY, PREP_QUANT = 3, 2, 4, 5
 W_HH_QUANT_SLOTS = (2, 5, 9, 7)
 W_HH_COPY_SLOT_VECTOR = 2
 W_HH_COPY_SLOT_SCALAR = 4
-GAIN_TURN_SLOT, GAIN_COPY_SLOT = 8, 10
-CELL_GAIN_SPREAD_SLOTS, CELL_GAIN_COPY_SLOTS = (12, 15), (13, 16)
-VECTOR_SHIFT_FROM_UNIT = UNITS - TURN_LAG
-VECTOR_SHIFT_TO_UNIT = UNITS - (TURN_LAG - NORM_LAG)
-VECTOR_AFFINE_FROM_TILE = TILES - 3
+GAIN_TURN_SLOT, GAIN_COPY_SLOT = 7, 8
+RATIO_SPREAD_SLOTS = (10, 12, 14, 16)
+CELL_GAIN_SPREAD_SLOTS, CELL_GAIN_COPY_SLOTS = (20, 24), (21, 25)
+TINY = 2.0 ** -60
+Y_RING = (5, 6, 6, 6)
 
 
 def cell_start(n):
@@ -80,9 +81,8 @@ def tile_layernormlstmcell_kernel(
     nc = tc.nc
     with ExitStack() as ctx:
         const = ctx.enter_context(tc.tile_pool(name="const", bufs=1))
-        wstage = ctx.enter_context(tc.tile_pool(name="wstage", bufs=4))
+        stage = ctx.enter_context(tc.tile_pool(name="stage", bufs=1))
         prep = ctx.enter_context(tc.tile_pool(name="prep", bufs=2))
-        ypool = ctx.enter_context(tc.tile_pool(name="ypool", bufs=12))
         gates = ctx.enter_context(tc.tile_pool(name="gates", bufs=2))
         cell = ctx.enter_context(tc.tile_pool(name="cell", bufs=3))
         small = ctx.enter_context(tc.tile_pool(name="small", bufs=3))
@@ -99,7 +99,7 @@ def tile_layernormlstmcell_kernel(
         w_raw = {}
 
         def load_w(m, q_lo, q_hi):
-            t = wstage.tile([P, PACK, (q_hi - q_lo) * BANK], BF16, name="w_raw", tag="w_raw", bufs=5)
+            t = stage.tile([P, PACK, (q_hi - q_lo) * BANK], BF16, name="w_raw_%d_%d" % (m, q_lo), offset=(4 * m + q_lo) * CHUNK_BYTES)
             nc.sync.dma_start(out=t[:], in_=w_views[m][:, :, q_lo * BANK:q_hi * BANK])
             for q in range(q_lo, q_hi):
                 w_raw[(m, q)] = t[:, :, (q - q_lo) * BANK:(q - q_lo + 1) * BANK]
@@ -126,11 +126,11 @@ def tile_layernormlstmcell_kernel(
         load_w(0, 1, 2)
         load_w(0, 2, 4)
         load_acts(2, 4)
-        load_w(1, 0, 2)
-        load_w(1, 2, 4)
         nc.vector.memset(gain_rows[:], 0.0)
         for i, vec in enumerate((gamma_ih, gamma_hh, beta_ih, beta_hh)):
             nc.sync.dma_start(out=gain_rows[GROUPS * i:GROUPS * (i + 1), :], in_=vec.rearrange("(j p) -> j p", p=P))
+        load_w(1, 0, 2)
+        load_w(1, 2, 4)
         nc.gpsimd.memset(cell_gain_row[:], 0.0)
         nc.sync.dma_start(out=cell_gain_row[0:1, 0:H], in_=gamma_c.rearrange("(o k) -> o k", o=1))
         nc.sync.dma_start(out=cell_gain_row[0:1, H:2 * H], in_=beta_c.rearrange("(o k) -> o k", o=1))
@@ -157,6 +157,11 @@ def tile_layernormlstmcell_kernel(
         beta_c_all = const.tile([P, H], BF16, name="beta_c_all", tag="beta_c_all")
         gain_cols = const.tile([P, 4 * GROUPS], F32, name="gain_cols", tag="gain_cols")
         beta_cols = const.tile([P, GROUPS], F32, name="beta_cols", tag="beta_cols")
+        near_zero = const.tile([P, GROUPS], F32, name="near_zero", tag="near_zero")
+        divisor = const.tile([P, GROUPS], F32, name="divisor", tag="divisor")
+        inverse = const.tile([P, GROUPS], F32, name="inverse", tag="inverse")
+        ratio_cols = const.tile([P, GROUPS], F32, name="ratio_cols", tag="ratio_cols")
+        ratio_all = const.tile([P, 4, BANK], F32, name="ratio_all", tag="ratio_all")
 
         w_codes = []
         w_scales = []
@@ -168,7 +173,7 @@ def tile_layernormlstmcell_kernel(
         w_grouped = {}
 
         def w_interleave(m, q, copy):
-            t = wstage.tile([P, BANK, PACK], BF16, name="w_grouped", tag="w_grouped", align_bytes=64)
+            t = stage.tile([P, BANK, PACK], BF16, name="w_grouped_%d_%d" % (m, q), offset=(8 + q) * CHUNK_BYTES)
             copy(
                 out=t[:].rearrange("p (c i) j -> p c j i", i=4),
                 in_=w_raw[(m, q)].rearrange("p j (c i) -> p c j i", i=4),
@@ -232,18 +237,6 @@ def tile_layernormlstmcell_kernel(
             )
             return acc
 
-        def norm_factors(mean_var, with_shift, tag, bufs):
-            t = small.tile([P, 4], F32, name=tag, tag=tag, bufs=bufs)
-            nc.gpsimd.tensor_scalar(
-                out=t[:, 0:1], in0=mean_var[:, 1:2], scalar1=1.0, scalar2=EPS, op0=ALU.mult, op1=ALU.add
-            )
-            nc.gpsimd.tensor_tensor(out=t[:, 1:2], in0=t[:, 0:1], in1=neg_half[:], op=ALU.pow)
-            if with_shift:
-                nc.gpsimd.tensor_scalar(
-                    out=t[:, 2:3], in0=mean_var[:, 0:1], scalar1=t[:, 1:2], scalar2=-1.0, op0=ALU.mult, op1=ALU.mult
-                )
-            return t
-
         scale_ps = ps_one.tile([P, K], F32, name="early", tag="early")
         nc.tensor.matmul(out=scale_ps[:], lhsT=ones_f32[:], rhs=scale_row[:], start=True, stop=True)
         nc.scalar.copy(out=scale_all[:], in_=scale_ps[:])
@@ -272,18 +265,17 @@ def tile_layernormlstmcell_kernel(
         stat_acc = {}
         norm_acc = {}
         stats = {}
+        moments = {}
         factors = {}
         y = {}
+        y_count = [0, 0, 0, 0]
         unit_ps = {}
-        shifted = {}
         gate = {}
         spread_ps = {}
         back_ps = {}
         f_c = {}
         c_new = {}
-        c_stats = {}
-        c_mean_var = {}
-        c_factors = {}
+        c_small = {}
         c_normed = {}
 
         def stat_piece(e):
@@ -294,9 +286,9 @@ def tile_layernormlstmcell_kernel(
 
         def norm_piece(i):
             pair, w = divmod(i, 16)
-            g, v = divmod(w, 4)
-            r, m = divmod(v, 2)
-            return pair, g, r, m
+            m, v = divmod(w, 8)
+            g, r = divmod(v, 2)
+            return 2 * pair + r, m, g
 
         def unit_place(u):
             pair, w = divmod(u, GROUPS)
@@ -307,44 +299,25 @@ def tile_layernormlstmcell_kernel(
             return gate[(pair, g)][:, 2 * half:2 * half + 2, :].rearrange("p j t -> p (j t)")
 
         def vector_slot(t):
-            u = t - TURN_LAG - 2
-            if 0 <= u < UNITS:
-                pair, g, jj, j = unit_place(u)
-                if jj == 0:
-                    tl = gates.tile([P, 4, 2 * P], F32, name="gate%d" % g, tag="gate%d" % g)
-                    gate[(pair, g)] = tl
-                nc.vector.scalar_tensor_tensor(
-                    out=gate[(pair, g)][:, jj, :],
-                    in0=unit_ps[u][:, 1, :, :].rearrange("p r t -> p (r t)"),
-                    scalar=gain_cols[:, GROUPS + j:GROUPS + j + 1],
-                    in1=shifted[u][:],
-                    op0=ALU.mult,
-                    op1=ALU.add,
-                )
-            u = t - TURN_LAG - 1
-            if VECTOR_SHIFT_FROM_UNIT <= u < VECTOR_SHIFT_TO_UNIT:
-                j = unit_place(u)[3]
-                tl = prep.tile([P, 2 * P], F32, name="shifted", tag="shifted", bufs=3)
-                nc.vector.tensor_scalar(
-                    out=tl[:],
-                    in0=unit_ps[u][:, 0, :, :].rearrange("p r t -> p (r t)"),
-                    scalar1=gain_cols[:, j:j + 1],
-                    scalar2=beta_cols[:, j:j + 1],
-                    op0=ALU.mult,
-                    op1=ALU.add,
-                )
-                shifted[u] = tl
             e = t - 1
             if 0 <= e < PIECES:
                 if e % 4 == 0:
                     tl = small.tile([P, 4, STATS_DIM], F32, name="stats", tag="stats")
                     stats[e // 4] = tl
                 nc.vector.bn_stats(out=stats[e // 4][:, e % 4, :], in_=stat_acc[e][:])
-            e = t - 2
+            e = t - 4
             if 0 <= e < PIECES and e % 4 == 3:
-                mean_var = small.tile([P, 2], F32, name="mean_var", tag="mean_var")
-                nc.vector.bn_aggr(out=mean_var[:], in_=stats[e // 4][:].rearrange("p q s -> p (q s)"))
-                factors[stat_piece(e)[0:2]] = norm_factors(mean_var, True, "factors", 10)
+                k = stat_piece(e)[0:2]
+                nc.vector.tensor_scalar(
+                    out=factors[k][:, 1:2], in0=moments[k][:, 0:1], scalar1=factors[k][:, 0:1], scalar2=-1.0, op0=ALU.mult, op1=ALU.mult
+                )
+            e = t - 1
+            if 0 <= e < PIECES and e % 4 == 3:
+                mv = small.tile([P, 4], F32, name="moments", tag="moments", bufs=4)
+                nc.vector.bn_aggr(out=mv[:, 0:2], in_=stats[e // 4][:].rearrange("p q s -> p (q s)"))
+                fac = small.tile([P, 2], F32, name="factors", tag="factors", bufs=6)
+                moments[stat_piece(e)[0:2]] = mv
+                factors[stat_piece(e)[0:2]] = fac
             for n in sorted(range(TILES), key=lambda i: (-cell_start(i), i)):
                 rows = slice(n * P, (n + 1) * P)
                 if t == cell_slot(n, F_C):
@@ -353,98 +326,97 @@ def tile_layernormlstmcell_kernel(
                     f_c[n] = tl
                 elif t == cell_slot(n, C_SUM):
                     tl = cell.tile([P, H], F32, name="c_new", tag="c_new")
-                    nc.vector.tensor_tensor(out=tl[:], in0=back_ps[("ig", n)][:], in1=f_c[n][:], op=ALU.add)
+                    sm = small.tile([P, 8], F32, name="c_small", tag="c_small", bufs=4)
+                    nc.vector.scalar_tensor_tensor(
+                        out=tl[:], in0=back_ps[("ig", n)][:], scalar=1.0, in1=f_c[n][:], op0=ALU.mult, op1=ALU.add, accum_out=sm[:, 0:1]
+                    )
                     nc.sync.dma_start(out=out_1[rows, :], in_=tl[:])
                     c_new[n] = tl
-                elif t == cell_slot(n, C_STATS):
-                    tl = small.tile([P, STATS_DIM], F32, name="c_stats", tag="c_stats")
-                    nc.vector.bn_stats(out=tl[:], in_=c_new[n][:])
-                    c_stats[n] = tl
-                elif t == cell_slot(n, C_AGGR):
-                    mean_var = small.tile([P, 2], F32, name="c_mean_var", tag="c_mean_var")
-                    nc.vector.bn_aggr(out=mean_var[:], in_=c_stats[n][:])
-                    on_gpsimd = n < VECTOR_AFFINE_FROM_TILE
-                    c_factors[n] = norm_factors(mean_var, on_gpsimd, "c_factors", 3)
+                    c_small[n] = sm
+                elif t == cell_slot(n, C_SUM) + 1:
+                    nc.vector.tensor_scalar(out=c_small[n][:, 1:2], in0=c_small[n][:, 0:1], scalar1=-1.0 / H, scalar2=0.0, op0=ALU.mult, op1=ALU.add)
+                if t == cell_slot(n, C_SQUARE) + 2:
+                    sm = c_small[n]
+                    nc.vector.tensor_scalar(out=sm[:, 3:4], in0=sm[:, 2:3], scalar1=1.0 / H, scalar2=EPS, op0=ALU.mult, op1=ALU.add)
+                    nc.gpsimd.tensor_tensor(out=sm[:, 4:5], in0=sm[:, 3:4], in1=neg_half[:], op=ALU.pow)
+                if t == cell_slot(n, C_GAIN):
                     tl = cell.tile([P, H], F32, name="c_normed", tag="c_normed")
-                    if on_gpsimd:
-                        nc.gpsimd.tensor_scalar(
-                            out=tl[:],
-                            in0=c_new[n][:],
-                            scalar1=c_factors[n][:, 1:2],
-                            scalar2=c_factors[n][:, 2:3],
-                            op0=ALU.mult,
-                            op1=ALU.add,
-                        )
-                    else:
-                        nc.vector.scalar_tensor_tensor(
-                            out=tl[:],
-                            in0=c_new[n][:],
-                            scalar=mean_var[:, 0:1],
-                            in1=gamma_c_all[:],
-                            op0=ALU.subtract,
-                            op1=ALU.mult,
-                        )
+                    nc.vector.scalar_tensor_tensor(
+                        out=tl[:], in0=c_new[n][:], scalar=c_small[n][:, 1:2], in1=gamma_c_all[:], op0=ALU.add, op1=ALU.mult
+                    )
                     c_normed[n] = tl
-                elif t == cell_slot(n, C_AFFINE):
+                elif t == cell_slot(n, C_SHIFT):
                     v = c_normed[n][:]
-                    if n < VECTOR_AFFINE_FROM_TILE:
-                        nc.gpsimd.tensor_tensor(out=v, in0=v, in1=gamma_c_all[:], op=ALU.mult)
-                        nc.gpsimd.tensor_tensor(out=v, in0=v, in1=beta_c_all[:], op=ALU.add)
-                    else:
-                        nc.vector.scalar_tensor_tensor(
-                            out=v, in0=v, scalar=c_factors[n][:, 1:2], in1=beta_c_all[:], op0=ALU.mult, op1=ALU.add
-                        )
+                    nc.vector.scalar_tensor_tensor(
+                        out=v, in0=v, scalar=c_small[n][:, 4:5], in1=beta_c_all[:], op0=ALU.mult, op1=ALU.add
+                    )
                 elif t == cell_slot(n, H_OUT):
                     tl = cell.tile([P, H], F32, name="h_new", tag="h_new")
                     nc.vector.tensor_tensor(out=tl[:], in0=back_ps[("o", n)][:], in1=c_normed[n][:], op=ALU.mult)
                     nc.sync.dma_start(out=out_0[rows, :], in_=tl[:])
-            pair, step = divmod(t - TURN_LAG, 16)
-            if 0 <= pair < PAIRS and step in IG_SLOTS:
-                half = IG_SLOTS.index(step)
-                iv = half_gate(pair, I_GATE, half)
-                nc.gpsimd.tensor_tensor(out=iv, in0=iv, in1=half_gate(pair, G_GATE, half), op=ALU.mult)
+            e = t - 1
+            if 0 <= e < PIECES and e % 4 == 3:
+                k = stat_piece(e)[0:2]
+                nc.vector.tensor_scalar(
+                    out=moments[k][:, 2:3], in0=moments[k][:, 1:2], scalar1=1.0, scalar2=EPS, op0=ALU.mult, op1=ALU.add
+                )
+                nc.gpsimd.tensor_tensor(out=factors[k][:, 0:1], in0=moments[k][:, 2:3], in1=neg_half[:], op=ALU.pow)
+            pair, step = divmod(t - NORM_LAG - 3, 16)
+            if 0 <= pair < PAIRS and step % 2 == 0:
+                g, r = divmod(step // 2, 2)
+                v = y[(pair, g, r, 0)][:]
+                nc.gpsimd.tensor_tensor(out=v, in0=v, in1=ratio_all[:, g, :], op=ALU.mult)
+            for half in range(2):
+                pair, step = divmod(t - TURN_LAG - IG_SLOTS[half], 16)
+                if step == 0 and 0 <= pair < PAIRS:
+                    iv = half_gate(pair, I_GATE, half)
+                    nc.gpsimd.tensor_tensor(out=iv, in0=iv, in1=half_gate(pair, G_GATE, half), op=ALU.mult)
             if t == W_HH_COPY_SLOT_VECTOR:
                 w_interleave(1, 3, nc.vector.tensor_copy)
             if t in W_HH_QUANT_SLOTS:
                 w_quantize(1, W_HH_QUANT_SLOTS.index(t))
-            period, place = divmod(t, 8)
-            if place == PREP_WIDEN and period + 3 < TILES:
-                a_widen(period + 3)
-            if place == PREP_QUANT and 2 <= period + 1 < TILES:
-                a_quantize(period + 1)
+            period, place = divmod(t - CELL_LAG % 8, 8)
+            if place == PREP_WIDEN and period + 3 + 0 < TILES and period + 3 + 0>=3:
+                a_widen(period + 3 + 0)
+            if place == PREP_QUANT and 2 <= period + 2 < TILES:
+                a_quantize(period + 2)
 
         def scalar_slot(t):
             u = t - TURN_LAG - 1
-            if 0 <= u < VECTOR_SHIFT_FROM_UNIT or VECTOR_SHIFT_TO_UNIT <= u < UNITS:
-                j = unit_place(u)[3]
-                tl = prep.tile([P, 2 * P], F32, name="shifted", tag="shifted", bufs=3)
+            if 0 <= u < UNITS:
+                pair, g, jj, j = unit_place(u)
+                if jj == 0:
+                    tl = gates.tile([P, 4, 2 * P], F32, name="gate%d" % g, tag="gate%d" % g)
+                    gate[(pair, g)] = tl
                 nc.scalar.activation(
-                    out=tl[:],
-                    in_=unit_ps[u][:, 0, :, :].rearrange("p r t -> p (r t)"),
-                    func=ACT.Identity,
+                    out=gate[(pair, g)][:, jj, :],
+                    in_=unit_ps[u][:].rearrange("p r t -> p (r t)"),
+                    func=(ACT.Tanh if g == G_GATE else ACT.Sigmoid),
                     bias=beta_cols[:, j:j + 1],
-                    scale=gain_cols[:, j:j + 1],
+                    scale=divisor[:, j:j + 1],
                 )
-                shifted[u] = tl
             i = t - NORM_LAG - 1
             if 0 <= i < PIECES:
-                pair, g, r, m = norm_piece(i)
-                fac = factors[(2 * pair + r, m)]
-                tl = ypool.tile([P, BANK], F32, name="y", tag="y")
-                nc.scalar.activation(
-                    out=tl[:], in_=norm_acc[i][:], func=ACT.Identity, bias=fac[:, 2:3], scale=fac[:, 1:2]
+                n, m, g = norm_piece(i)
+                fac = factors[(n, m)]
+                k = y_count[g]
+                tl = stage.tile(
+                    [P, BANK], F32, name="y_%d_%d" % (g, k), offset=(sum(Y_RING[:g]) + k % Y_RING[g]) * BANK * 4
                 )
-                y[(pair, g, r, m)] = tl
-            pair, step = divmod(t - TURN_LAG - 3, 16)
-            if 0 <= pair < PAIRS and step % 2 == 0:
-                g, half = divmod(step // 2, 2)
-                v = half_gate(pair, g, half)
-                nc.scalar.activation(out=v, in_=v, func=(ACT.Tanh if g == G_GATE else ACT.Sigmoid))
+                y_count[g] = k + 1
+                nc.scalar.activation(
+                    out=tl[:], in_=norm_acc[i][:], func=ACT.Identity, bias=fac[:, 1:2], scale=fac[:, 0:1]
+                )
+                y[(n // 2, g, n % 2, m)] = tl
             for n in range(TILES):
+                if t == cell_slot(n, C_SQUARE):
+                    sm = c_small[n]
+                    sq = cell.tile([P, H], F32, name="square", tag="square", bufs=2)
+                    nc.scalar.activation(out=sq[:], in_=c_new[n][:], func=ACT.Square, bias=sm[:, 1:2], accum_out=sm[:, 2:3])
                 if t == cell_slot(n, C_TANH):
                     nc.scalar.activation(out=c_normed[n][:], in_=c_normed[n][:], func=ACT.Tanh)
-            period, place = divmod(t, 8)
-            if place == PREP_COPY and period + 2 < TILES:
+            period, place = divmod(t - CELL_LAG % 8, 8)
+            if place == PREP_COPY and 2 <= period + 2 < TILES:
                 a_copy(period + 2)
             if t == W_HH_COPY_SLOT_SCALAR:
                 w_interleave(1, 2, nc.scalar.copy)
@@ -456,6 +428,20 @@ def tile_layernormlstmcell_kernel(
                     in1=gain_cols[:, 3 * GROUPS:4 * GROUPS],
                     op=ALU.add,
                 )
+                gamma_hh_cols = gain_cols[:, GROUPS:2 * GROUPS]
+                nc.gpsimd.tensor_scalar(
+                    out=near_zero[:], in0=gamma_hh_cols, scalar1=TINY, scalar2=2.0 * TINY, op0=ALU.is_lt, op1=ALU.mult
+                )
+                nc.gpsimd.tensor_scalar(
+                    out=divisor[:], in0=gamma_hh_cols, scalar1=-TINY, scalar2=1.0, op0=ALU.is_gt, op1=ALU.mult
+                )
+                nc.gpsimd.tensor_tensor(out=near_zero[:], in0=near_zero[:], in1=divisor[:], op=ALU.mult)
+                nc.gpsimd.tensor_tensor(out=divisor[:], in0=gamma_hh_cols, in1=near_zero[:], op=ALU.add)
+                nc.vector.reciprocal(out=inverse[:], in_=divisor[:])
+                nc.gpsimd.tensor_tensor(out=ratio_cols[:], in0=gain_cols[:, 0:GROUPS], in1=inverse[:], op=ALU.mult)
+            elif t - 1 in RATIO_SPREAD_SLOTS:
+                g = RATIO_SPREAD_SLOTS.index(t - 1)
+                nc.scalar.copy(out=ratio_all[:, g, :], in_=spread_ps[("ratio", g)][:].rearrange("p i c -> p (i c)"))
             elif t in CELL_GAIN_COPY_SLOTS:
                 which = CELL_GAIN_COPY_SLOTS.index(t)
                 nc.scalar.copy(out=(gamma_c_all, beta_c_all)[which][:], in_=spread_ps[which][:])
@@ -475,11 +461,20 @@ def tile_layernormlstmcell_kernel(
                     ident[:],
                 )
 
-        def tensor_slot(t):
+        def turn_slot(t):
             if t == GAIN_TURN_SLOT:
                 tl = ps_one.tile([P, P], BF16, name="early", tag="early")
                 nc.tensor.transpose(tl[:], gain_rows[:], ident_bf16[:])
                 spread_ps["gains"] = tl
+            elif t in RATIO_SPREAD_SLOTS:
+                g = RATIO_SPREAD_SLOTS.index(t)
+                tl = ps_unit.tile([P, 4, P], F32, name="unit_ps", tag="unit_ps")
+                for jj in range(4):
+                    j = 4 * GATE_ORDER[g] + jj
+                    nc.tensor.matmul(
+                        out=tl[:, jj, :], lhsT=ratio_cols[:, j:j + 1].to_broadcast([P, P]), rhs=ident[:], start=True, stop=True
+                    )
+                spread_ps[("ratio", g)] = tl
             elif t in CELL_GAIN_SPREAD_SLOTS:
                 which = CELL_GAIN_SPREAD_SLOTS.index(t)
                 tl = ps_one.tile([P, H], F32, name="early", tag="early")
@@ -491,26 +486,40 @@ def tile_layernormlstmcell_kernel(
                 for what, g, step in (("f", F_GATE, F_TURN), ("ig", I_GATE, IG_TURN), ("o", O_GATE, O_TURN)):
                     if t - cell_slot(n, step) in (0, 1):
                         turn_back(what, n, g, t - cell_slot(n, step))
-            period, place = divmod(t, 8)
-            if place in (2, 3) and period + 2 < TILES:
-                a_turn(period + 2, place % 2)
+            period, place = divmod(t - CELL_LAG % 8, 8)
+            if place in (PREP_TURN, PREP_TURN + 1) and 2 <= period + 2 < TILES:
+                a_turn(period + 2, place - PREP_TURN)
+            u = t - TURN_LAG
+            if 0 <= u < UNITS:
+                pair, g, jj, j = unit_place(u)
+                tl = ps_unit.tile([P, 2, P], F32, name="unit_ps", tag="unit_ps")
+                for r in range(2):
+                    for m in range(2):
+                        nc.tensor.matmul(
+                            out=tl[:, r, :],
+                            lhsT=y[(pair, g, r, m)][:, jj * P:(jj + 1) * P],
+                            rhs=ident[:],
+                            is_transpose=True,
+                            start=(m == 0),
+                            stop=(m == 1),
+                        )
+                unit_ps[u] = tl
+
+        def product_slot(t):
             if t < PIECES:
                 n, m, q = stat_piece(t)
                 stat_acc[t] = product_piece(ps_stat, "stat_acc", n, m, q)
             i = t - NORM_LAG
             if 0 <= i < PIECES:
-                pair, g, r, m = norm_piece(i)
-                norm_acc[i] = product_piece(ps_norm, "norm_acc", 2 * pair + r, m, GATE_ORDER[g])
-            u = t - TURN_LAG
-            if 0 <= u < UNITS:
-                pair, g, jj, j = unit_place(u)
-                tl = ps_unit.tile([P, 2, 2, P], F32, name="unit_ps", tag="unit_ps")
-                for m in range(2):
-                    for r in range(2):
-                        nc.tensor.transpose(tl[:, m, r, :], y[(pair, g, r, m)][:, jj * P:(jj + 1) * P], ident[:])
-                unit_ps[u] = tl
+                n, m, g = norm_piece(i)
+                norm_acc[i] = product_piece(ps_norm, "norm_acc", n, m, GATE_ORDER[g])
 
         for t in range(LAST_SLOT + 1):
             vector_slot(t)
             scalar_slot(t)
-            tensor_slot(t)
+            if t % 2 == 0:
+                turn_slot(t)
+                product_slot(t)
+            else:
+                product_slot(t)
+                turn_slot(t)

@@ -34,31 +34,59 @@ TURN_LAG = NORM_LAG + 11
 CELL_LAG = TURN_LAG + 13
 F_TURN, F_C, IG_TURN, C_SUM, C_SQUARE, C_GAIN, C_SHIFT, C_TANH, O_TURN, H_OUT = 0, 1, 2, 3, 4, 5, 6, 7, 8, 9
 CELL_STEPS = (0, 2, 4, 6, 7, 9, 12, 14, 14, 16)
-LAST_CELL_STEPS = (0, 2, 2, 4, 6, 6, 9, 10, 4, 12)
-LAST_CELL_LEAD = 0
+LAST_CELL_STEPS = (0, 1, 1, 2, 3, 4, 6, 7, 3, 8)
+MID_CELL_SLOT = CELL_LAG + 8 * (TILES - 4) - 0
+MID_CELL_STEPS = (0, 1, 2, 3, 4, 5, 7, 8, 8, 10)
+LAST_NORM_SLOT = 131
+LAST_UNIT_SLOT = LAST_NORM_SLOT + 2
+LAST_CELL_SLOT = LAST_UNIT_SLOT + 6
 IG_SLOTS = (8, 13)
+LAST_IG_SLOTS = (4, 5)
+RATIO_LAG = 4
 PREP_WIDEN, PREP_TURN, PREP_COPY, PREP_QUANT = 3, 2, 4, 5
-W_HH_QUANT_SLOTS = (2, 5, 9, 7)
-W_HH_COPY_SLOT_VECTOR = 2
-W_HH_COPY_SLOT_SCALAR = 4
 GAIN_TURN_SLOT, GAIN_COPY_SLOT = 7, 8
-RATIO_SPREAD_SLOTS = (10, 12, 14, 16)
-CELL_GAIN_SPREAD_SLOTS, CELL_GAIN_COPY_SLOTS = (20, 24), (21, 25)
+RATIO_SPREAD_SLOTS = (12, 14, 16, 18)
+CELL_GAIN_SPREAD_SLOTS, CELL_GAIN_COPY_SLOTS = (20, 22), (21, 23)
 TINY = 2.0 ** -60
-Y_RING = (5, 6, 6, 6)
+Y_RING = (6, 7, 8, 8)
+
+
+def norm_slot(i):
+    if i < PIECES - 8:
+        return i + NORM_LAG
+    return LAST_NORM_SLOT + (i - (PIECES - 8)) // 4
+
+
+def unit_slot(u):
+    if u < UNITS - GROUPS:
+        return u + TURN_LAG
+    return LAST_UNIT_SLOT + (u - (UNITS - GROUPS)) // 2
+
+
+def ratio_slot(pair, k):
+    return 16 * pair + NORM_LAG + RATIO_LAG + (2 * k if pair < PAIRS - 1 else k)
+
+
+def ig_slot(pair, half):
+    if pair < PAIRS - 1:
+        return 16 * pair + TURN_LAG + IG_SLOTS[half]
+    return LAST_UNIT_SLOT + LAST_IG_SLOTS[half]
 
 
 def cell_start(n):
-    if n < TILES - 2:
+    if n < TILES - 4:
         return CELL_LAG + 8 * n
-    return CELL_LAG + 8 * (TILES - 2) - LAST_CELL_LEAD
+    if n < TILES - 2:
+        return MID_CELL_SLOT + n % 2
+    return LAST_CELL_SLOT
 
 
 def cell_slot(n, step):
-    return cell_start(n) + (CELL_STEPS if n < TILES - 2 else LAST_CELL_STEPS)[step]
+    steps = CELL_STEPS if n < TILES - 4 else MID_CELL_STEPS if n < TILES - 2 else LAST_CELL_STEPS
+    return cell_start(n) + steps[step]
 
 
-LAST_SLOT = CELL_LAG + 8 * (TILES - 2) - LAST_CELL_LEAD + LAST_CELL_STEPS[H_OUT]
+LAST_SLOT = max(cell_slot(n, H_OUT) for n in range(TILES))
 
 
 def tile_layernormlstmcell_kernel(
@@ -93,8 +121,8 @@ def tile_layernormlstmcell_kernel(
         ctx.enter_context(tc.manual_schedule())
 
         w_views = (
-            W_ih.rearrange("(p j) w -> p j w", j=PACK),
             W_hh.rearrange("(p j) w -> p j w", j=PACK),
+            W_ih.rearrange("(p j) w -> p j w", j=PACK),
         )
         w_raw = {}
 
@@ -111,31 +139,38 @@ def tile_layernormlstmcell_kernel(
         h_view = h_prev.rearrange("(n p) k -> p n k", p=P)
         c_view = c_prev.rearrange("(n p) k -> p n k", p=P)
 
-        def load_acts(lo, hi):
+        def load_x(lo, hi):
             nc.sync.dma_start(out=x_sb[:, lo:hi, :], in_=x_view[:, lo:hi, :])
+
+        def load_h(lo, hi):
             nc.sync.dma_start(out=h_sb[:, lo:hi, :], in_=h_view[:, lo:hi, :])
 
         scale_row = const.tile([P, K], F32, name="scale_row", tag="scale_row")
         cell_gain_row = const.tile([P, 2 * H], BF16, name="cell_gain_row", tag="cell_gain_row")
         gain_rows = const.tile([P, P], BF16, name="gain_rows", tag="gain_rows")
+        ident = const.tile([P, P], F32, name="ident", tag="ident")
 
+        load_h(0, 2)
         load_w(0, 0, 1)
+        load_w(0, 1, 2)
+        make_identity(nc, ident[:])
         nc.gpsimd.memset(scale_row[:], 0.0)
         nc.sync.dma_start(out=scale_row[0:1, :], in_=x_scale)
-        load_acts(0, 2)
-        load_w(0, 1, 2)
+        load_x(0, 2)
         load_w(0, 2, 4)
-        load_acts(2, 4)
         nc.vector.memset(gain_rows[:], 0.0)
-        for i, vec in enumerate((gamma_ih, gamma_hh, beta_ih, beta_hh)):
+        for i, vec in enumerate((gamma_hh, gamma_ih, beta_hh, beta_ih)):
             nc.sync.dma_start(out=gain_rows[GROUPS * i:GROUPS * (i + 1), :], in_=vec.rearrange("(j p) -> j p", p=P))
+        load_h(2, 4)
+        load_x(2, 4)
         load_w(1, 0, 2)
         load_w(1, 2, 4)
         nc.gpsimd.memset(cell_gain_row[:], 0.0)
         nc.sync.dma_start(out=cell_gain_row[0:1, 0:H], in_=gamma_c.rearrange("(o k) -> o k", o=1))
         nc.sync.dma_start(out=cell_gain_row[0:1, H:2 * H], in_=beta_c.rearrange("(o k) -> o k", o=1))
         for lo in (4, 8, 12):
-            load_acts(lo, lo + 4)
+            load_h(lo, lo + 4)
+            load_x(lo, lo + 4)
         for lo in (0, 4, 8, 12):
             nc.sync.dma_start(out=c_sb[:, lo:lo + 4, :], in_=c_view[:, lo:lo + 4, :])
 
@@ -144,13 +179,11 @@ def tile_layernormlstmcell_kernel(
         warm = const.tile([P, 1], F32, name="warm", tag="warm")
         nc.gpsimd.memset(warm[:], 0.0)
         nc.scalar.activation(out=warm[:], in_=warm[:], func=ACT.Sigmoid)
-        ident = const.tile([P, P], F32, name="ident", tag="ident")
-        make_identity(nc, ident[:])
         ident_bf16 = const.tile([P, P], BF16, name="ident_bf16", tag="ident_bf16")
         make_identity(nc, ident_bf16[:])
         ones_bf16 = const.tile([P, P], BF16, name="ones_bf16", tag="ones_bf16")
         nc.gpsimd.memset(ones_bf16[:], 1.0)
-        neg_half = const.tile([P, 1], F32, name="neg_half", tag="neg_half")
+        neg_half = const.tile([P, 2], F32, name="neg_half", tag="neg_half")
         nc.gpsimd.memset(neg_half[:], -0.5)
         scale_all = const.tile([P, K], F32, name="scale_all", tag="scale_all")
         gamma_c_all = const.tile([P, H], BF16, name="gamma_c_all", tag="gamma_c_all")
@@ -189,47 +222,46 @@ def tile_layernormlstmcell_kernel(
             )
 
         x_bf16 = {}
-        turned = {}
-        a_grouped = {}
-        a_codes = {}
-        a_scales = {}
+        operand = {}
 
         def a_widen(n):
             t = prep.tile([P, K], BF16, name="x_bf16", tag="x_bf16", bufs=3)
             nc.vector.tensor_tensor(out=t[:], in0=x_sb[:, n, :].bitcast(FP8), in1=scale_all[:], op=ALU.mult)
             x_bf16[n] = t
 
-        def a_turn(n, m):
-            if m == 0:
-                t = ps_one.tile([P, 2 * 2, P], F32, name="late", tag="late")
-                turned[n] = t
-            words = (x_bf16[n][:] if m == 0 else h_sb[:, n, :]).bitcast(F32)
+        def a_turn(bank, place, n, m):
+            words = (h_sb[:, n, :] if m == 0 else x_bf16[n][:]).bitcast(F32)
             for u in range(2):
-                nc.tensor.transpose(turned[n][:, 2 * m + u, :], words[:, u:K // 2:2], ident[:])
+                nc.tensor.transpose(bank[:, 2 * place + u, :], words[:, u:K // 2:2], ident[:])
 
-        def a_copy(n):
+        def turn_bank():
+            t = ps_one.tile([P, 2 * 2, P], F32, name="late", tag="late")
+            return t
+
+        def a_copy(bank, copy):
             t = prep.tile([P, 2 * P * PACK], BF16, name="a_grouped", tag="a_grouped", align_bytes=64)
-            nc.scalar.copy(
-                out=t[:].bitcast(F32).rearrange("p (m r u) -> p m r u", m=2, u=2),
-                in_=turned[n][:].rearrange("p (m u) r -> p m r u", u=2),
+            copy(
+                out=t[:].bitcast(F32).rearrange("p (o r u) -> p o r u", o=2, u=2),
+                in_=bank[:].rearrange("p (o u) r -> p o r u", u=2),
             )
-            a_grouped[n] = t
+            return t
 
-        def a_quantize(n):
+        def a_quantize(grouped, places):
             codes = prep.tile([P, 2 * P], U32, name="a_codes", tag="a_codes", bufs=8, align_bytes=64)
             scales = prep.tile([P, 2 * P], U8, name="a_scales", tag="a_scales", bufs=8, align_bytes=64)
-            nc.vector.quantize_mx(out=codes[:].bitcast(FP8X4), scales=scales[:], in_=a_grouped[n][:])
-            a_codes[n] = codes
-            a_scales[n] = scales
+            nc.vector.quantize_mx(out=codes[:].bitcast(FP8X4), scales=scales[:], in_=grouped[:])
+            for place, key in enumerate(places):
+                cols = slice(place * P, (place + 1) * P)
+                operand[key] = (codes[:, cols], scales[:, cols])
 
         def product_piece(pool, tag, n, m, q):
-            tokens = slice(m * P, (m + 1) * P)
             cols = slice(q * BANK, (q + 1) * BANK)
+            codes, scales = operand[(n, m)]
             acc = pool.tile([P, BANK], F32, name=tag, tag=tag)
             nc.tensor.matmul_mx(
                 out=acc[:],
-                lhsT=a_codes[n][:, tokens].bitcast(FP8X4),
-                lhsT_scale=a_scales[n][:, tokens],
+                lhsT=codes.bitcast(FP8X4),
+                lhsT_scale=scales,
                 rhs=w_codes[m][:, cols].bitcast(FP8X4),
                 rhs_scale=w_scales[m][:, cols],
                 start=True,
@@ -237,30 +269,18 @@ def tile_layernormlstmcell_kernel(
             )
             return acc
 
-        scale_ps = ps_one.tile([P, K], F32, name="early", tag="early")
+        head = {}
+        h_bank = turn_bank()
+        a_turn(h_bank, 0, 0, 0)
+        a_turn(h_bank, 1, 1, 0)
+        scale_ps = ps_unit.tile([P, K], F32, name="unit_ps", tag="unit_ps")
         nc.tensor.matmul(out=scale_ps[:], lhsT=ones_f32[:], rhs=scale_row[:], start=True, stop=True)
+        head["h"] = a_copy(h_bank, nc.scalar.copy)
         nc.scalar.copy(out=scale_all[:], in_=scale_ps[:])
         w_interleave(0, 0, nc.vector.tensor_copy)
-        a_widen(0)
-        w_interleave(0, 1, nc.scalar.copy)
-        a_turn(0, 0)
-        a_turn(0, 1)
-        a_widen(1)
+        a_quantize(head["h"], ((0, 0), (1, 0)))
         w_quantize(0, 0)
-        w_interleave(0, 2, nc.vector.tensor_copy)
-        a_copy(0)
-        w_interleave(0, 3, nc.scalar.copy)
-        w_quantize(0, 1)
-        a_turn(1, 0)
-        a_turn(1, 1)
-        a_quantize(0)
-        w_quantize(0, 2)
-        a_copy(1)
-        a_widen(2)
-        w_quantize(0, 3)
-        a_quantize(1)
-        w_interleave(1, 0, nc.scalar.copy)
-        w_interleave(1, 1, nc.scalar.copy)
+        w_interleave(0, 1, nc.vector.tensor_copy)
 
         stat_acc = {}
         norm_acc = {}
@@ -273,6 +293,8 @@ def tile_layernormlstmcell_kernel(
         gate = {}
         spread_ps = {}
         back_ps = {}
+        turned = {}
+        grouped = {}
         f_c = {}
         c_new = {}
         c_small = {}
@@ -281,14 +303,14 @@ def tile_layernormlstmcell_kernel(
         def stat_piece(e):
             pair, w = divmod(e, 16)
             m, v = divmod(w, 8)
-            r, q = divmod(v, 4)
-            return 2 * pair + r, m, q
+            q, r = divmod(v, 2)
+            return pair, m, q, r
 
         def norm_piece(i):
             pair, w = divmod(i, 16)
             m, v = divmod(w, 8)
             g, r = divmod(v, 2)
-            return 2 * pair + r, m, g
+            return pair, m, g, r
 
         def unit_place(u):
             pair, w = divmod(u, GROUPS)
@@ -298,26 +320,72 @@ def tile_layernormlstmcell_kernel(
         def half_gate(pair, g, half):
             return gate[(pair, g)][:, 2 * half:2 * half + 2, :].rearrange("p j t -> p (j t)")
 
+        def y_tile(g):
+            k = y_count[g]
+            y_count[g] = k + 1
+            tl = stage.tile([P, BANK], F32, name="y_%d_%d" % (g, k), offset=(sum(Y_RING[:g]) + k % Y_RING[g]) * BANK * 4)
+            return tl
+
+        def ratio_on_vector(pair, g, r):
+            return r == 1 and pair == PAIRS - 1
+
+        def norm_on_vector(pair, m, g, r):
+            return pair == PAIRS - 1 and m == 1 and r == 1
+
+        norm_at = {}
+        for i in range(PIECES):
+            norm_at.setdefault(norm_slot(i), []).append(i)
+        unit_at = {}
+        for u in range(UNITS):
+            unit_at.setdefault(unit_slot(u), []).append(u)
+        ratio_at = {}
+        for pair in range(PAIRS):
+            for k in range(8):
+                ratio_at.setdefault(ratio_slot(pair, k), []).append((pair, k // 2, k % 2))
+        ig_at = {}
+        for pair in range(PAIRS):
+            for half in range(2):
+                ig_at.setdefault(ig_slot(pair, half), []).append((pair, half))
+
         def vector_slot(t):
             e = t - 1
             if 0 <= e < PIECES:
-                if e % 4 == 0:
-                    tl = small.tile([P, 4, STATS_DIM], F32, name="stats", tag="stats")
-                    stats[e // 4] = tl
-                nc.vector.bn_stats(out=stats[e // 4][:, e % 4, :], in_=stat_acc[e][:])
+                pair, m, q, r = stat_piece(e)
+                if e % 8 == 0:
+                    tl = small.tile([P, 2, 4, STATS_DIM], F32, name="stats", tag="stats")
+                    stats[(pair, m)] = tl
+                nc.vector.bn_stats(out=stats[(pair, m)][:, r, q, :], in_=stat_acc[e][:])
+            for i in norm_at.get(t - 1, ()):
+                pair, m, g, r = norm_piece(i)
+                if m == 0 and ratio_on_vector(pair, g, r):
+                    tl = y_tile(g)
+                    nc.vector.scalar_tensor_tensor(
+                        out=tl[:], in0=norm_acc[i][:], scalar=moments[(pair, m)][:, 2 * r:2 * r + 1], in1=ratio_all[:, g, :],
+                        op0=ALU.subtract, op1=ALU.mult,
+                    )
+                    y[(pair, g, r, m)] = tl
+                elif norm_on_vector(pair, m, g, r):
+                    fac = factors[(pair, m)]
+                    tl = y_tile(g)
+                    nc.vector.tensor_scalar(
+                        out=tl[:], in0=norm_acc[i][:], scalar1=fac[:, r:r + 1], scalar2=fac[:, 2 + r:3 + r], op0=ALU.mult, op1=ALU.add
+                    )
+                    y[(pair, g, r, m)] = tl
             e = t - 4
-            if 0 <= e < PIECES and e % 4 == 3:
+            if 0 <= e < PIECES and e % 8 == 7:
                 k = stat_piece(e)[0:2]
-                nc.vector.tensor_scalar(
-                    out=factors[k][:, 1:2], in0=moments[k][:, 0:1], scalar1=factors[k][:, 0:1], scalar2=-1.0, op0=ALU.mult, op1=ALU.mult
+                nc.vector.scalar_tensor_tensor(
+                    out=factors[k][:, 2:4], in0=moments[k][:, 0:4:2], scalar=-1.0, in1=factors[k][:, 0:2], op0=ALU.mult, op1=ALU.mult
                 )
             e = t - 1
-            if 0 <= e < PIECES and e % 4 == 3:
-                mv = small.tile([P, 4], F32, name="moments", tag="moments", bufs=4)
-                nc.vector.bn_aggr(out=mv[:, 0:2], in_=stats[e // 4][:].rearrange("p q s -> p (q s)"))
-                fac = small.tile([P, 2], F32, name="factors", tag="factors", bufs=6)
-                moments[stat_piece(e)[0:2]] = mv
-                factors[stat_piece(e)[0:2]] = fac
+            if 0 <= e < PIECES and e % 8 == 7:
+                k = stat_piece(e)[0:2]
+                mv = small.tile([P, 8], F32, name="moments", tag="moments", bufs=4)
+                for r in range(2):
+                    nc.vector.bn_aggr(out=mv[:, 2 * r:2 * r + 2], in_=stats[k][:, r, :, :].rearrange("p q s -> p (q s)"))
+                fac = small.tile([P, 4], F32, name="factors", tag="factors", bufs=4)
+                moments[k] = mv
+                factors[k] = fac
             for n in sorted(range(TILES), key=lambda i: (-cell_start(i), i)):
                 rows = slice(n * P, (n + 1) * P)
                 if t == cell_slot(n, F_C):
@@ -335,10 +403,10 @@ def tile_layernormlstmcell_kernel(
                     c_small[n] = sm
                 elif t == cell_slot(n, C_SUM) + 1:
                     nc.vector.tensor_scalar(out=c_small[n][:, 1:2], in0=c_small[n][:, 0:1], scalar1=-1.0 / H, scalar2=0.0, op0=ALU.mult, op1=ALU.add)
-                if t == cell_slot(n, C_SQUARE) + 2:
+                if t == cell_slot(n, C_SQUARE) + (2 if n < TILES - 4 else 1):
                     sm = c_small[n]
                     nc.vector.tensor_scalar(out=sm[:, 3:4], in0=sm[:, 2:3], scalar1=1.0 / H, scalar2=EPS, op0=ALU.mult, op1=ALU.add)
-                    nc.gpsimd.tensor_tensor(out=sm[:, 4:5], in0=sm[:, 3:4], in1=neg_half[:], op=ALU.pow)
+                    nc.gpsimd.tensor_tensor(out=sm[:, 4:5], in0=sm[:, 3:4], in1=neg_half[:, 0:1], op=ALU.pow)
                 if t == cell_slot(n, C_GAIN):
                     tl = cell.tile([P, H], F32, name="c_normed", tag="c_normed")
                     nc.vector.scalar_tensor_tensor(
@@ -355,35 +423,57 @@ def tile_layernormlstmcell_kernel(
                     nc.vector.tensor_tensor(out=tl[:], in0=back_ps[("o", n)][:], in1=c_normed[n][:], op=ALU.mult)
                     nc.sync.dma_start(out=out_0[rows, :], in_=tl[:])
             e = t - 1
-            if 0 <= e < PIECES and e % 4 == 3:
+            if 0 <= e < PIECES and e % 8 == 7:
                 k = stat_piece(e)[0:2]
                 nc.vector.tensor_scalar(
-                    out=moments[k][:, 2:3], in0=moments[k][:, 1:2], scalar1=1.0, scalar2=EPS, op0=ALU.mult, op1=ALU.add
+                    out=moments[k][:, 4:6], in0=moments[k][:, 1:4:2], scalar1=1.0, scalar2=EPS, op0=ALU.mult, op1=ALU.add
                 )
-                nc.gpsimd.tensor_tensor(out=factors[k][:, 0:1], in0=moments[k][:, 2:3], in1=neg_half[:], op=ALU.pow)
-            pair, step = divmod(t - NORM_LAG - 3, 16)
-            if 0 <= pair < PAIRS and step % 2 == 0:
-                g, r = divmod(step // 2, 2)
-                v = y[(pair, g, r, 0)][:]
-                nc.gpsimd.tensor_tensor(out=v, in0=v, in1=ratio_all[:, g, :], op=ALU.mult)
-            for half in range(2):
-                pair, step = divmod(t - TURN_LAG - IG_SLOTS[half], 16)
-                if step == 0 and 0 <= pair < PAIRS:
-                    iv = half_gate(pair, I_GATE, half)
-                    nc.gpsimd.tensor_tensor(out=iv, in0=iv, in1=half_gate(pair, G_GATE, half), op=ALU.mult)
-            if t == W_HH_COPY_SLOT_VECTOR:
-                w_interleave(1, 3, nc.vector.tensor_copy)
-            if t in W_HH_QUANT_SLOTS:
-                w_quantize(1, W_HH_QUANT_SLOTS.index(t))
+                nc.gpsimd.tensor_tensor(out=factors[k][:, 0:2], in0=moments[k][:, 4:6], in1=neg_half[:], op=ALU.pow)
+            for pair, g, r in ratio_at.get(t, ()):
+                if not ratio_on_vector(pair, g, r):
+                    v = y[(pair, g, r, 0)][:]
+                    nc.gpsimd.tensor_tensor(out=v, in0=v, in1=ratio_all[:, g, :], op=ALU.mult)
+            for pair, half in ig_at.get(t, ()):
+                iv = half_gate(pair, I_GATE, half)
+                nc.gpsimd.tensor_tensor(out=iv, in0=iv, in1=half_gate(pair, G_GATE, half), op=ALU.mult)
+            for what, m, q in HEAD_VECTOR.get(t, ()):
+                if what == "interleave":
+                    w_interleave(m, q, nc.vector.tensor_copy)
+                elif what == "quantize":
+                    w_quantize(m, q)
+                elif what == "widen":
+                    a_widen(q)
+                else:
+                    a_quantize(head["x"], ((0, 1), (1, 1)))
             period, place = divmod(t - CELL_LAG % 8, 8)
-            if place == PREP_WIDEN and period + 3 + 0 < TILES and period + 3 + 0>=3:
-                a_widen(period + 3 + 0)
+            if place == PREP_WIDEN and 2 <= period + 3 < TILES:
+                a_widen(period + 3)
             if place == PREP_QUANT and 2 <= period + 2 < TILES:
-                a_quantize(period + 2)
+                n = period + 2
+                a_quantize(grouped[n], ((n, 0), (n, 1)))
 
-        def scalar_slot(t):
-            u = t - TURN_LAG - 1
-            if 0 <= u < UNITS:
+        HEAD_VECTOR = {
+            1: (("quantize", 0, 1),),
+            2: (("widen", 1, 0), ("widen", 1, 1)),
+            3: (("quantize", 0, 2),),
+            4: (("widen", 1, 2),),
+            5: (("quantize", 0, 3),),
+            7: (("x", 0, 0), ("quantize", 1, 0)),
+            9: (("quantize", 1, 1),),
+            11: (("quantize", 1, 2),),
+            13: (("quantize", 1, 3),),
+        }
+        HEAD_SCALAR = {
+            1: (("interleave", 0, 2), ("interleave", 0, 3)),
+            4: (("x", 0, 0), ("interleave", 1, 0)),
+            6: (("interleave", 1, 1),),
+            8: (("interleave", 1, 2),),
+            10: (("interleave", 1, 3),),
+        }
+        HEAD_TENSOR = {3: "x"}
+
+        def finish_gate(t):
+            for u in unit_at.get(t - 1, ()):
                 pair, g, jj, j = unit_place(u)
                 if jj == 0:
                     tl = gates.tile([P, 4, 2 * P], F32, name="gate%d" % g, tag="gate%d" % g)
@@ -395,19 +485,30 @@ def tile_layernormlstmcell_kernel(
                     bias=beta_cols[:, j:j + 1],
                     scale=divisor[:, j:j + 1],
                 )
-            i = t - NORM_LAG - 1
-            if 0 <= i < PIECES:
-                n, m, g = norm_piece(i)
-                fac = factors[(n, m)]
-                k = y_count[g]
-                tl = stage.tile(
-                    [P, BANK], F32, name="y_%d_%d" % (g, k), offset=(sum(Y_RING[:g]) + k % Y_RING[g]) * BANK * 4
-                )
-                y_count[g] = k + 1
-                nc.scalar.activation(
-                    out=tl[:], in_=norm_acc[i][:], func=ACT.Identity, bias=fac[:, 1:2], scale=fac[:, 0:1]
-                )
-                y[(n // 2, g, n % 2, m)] = tl
+
+        def normalise(t):
+            for i in norm_at.get(t - 2, ()):
+                pair, m, g, r = norm_piece(i)
+                if m == 0 and ratio_on_vector(pair, g, r):
+                    v = y[(pair, g, r, m)][:]
+                    nc.scalar.activation(out=v, in_=v, func=ACT.Copy, scale=factors[(pair, m)][:, r:r + 1])
+            for i in norm_at.get(t - 1, ()):
+                pair, m, g, r = norm_piece(i)
+                if not (m == 0 and ratio_on_vector(pair, g, r)) and not norm_on_vector(pair, m, g, r):
+                    fac = factors[(pair, m)]
+                    tl = y_tile(g)
+                    nc.scalar.activation(
+                        out=tl[:], in_=norm_acc[i][:], func=ACT.Identity, bias=fac[:, 2 + r:3 + r], scale=fac[:, r:r + 1]
+                    )
+                    y[(pair, g, r, m)] = tl
+
+        def scalar_slot(t):
+            if t % 2 == 0:
+                normalise(t)
+                finish_gate(t)
+            else:
+                finish_gate(t)
+                normalise(t)
             for n in range(TILES):
                 if t == cell_slot(n, C_SQUARE):
                     sm = c_small[n]
@@ -415,11 +516,14 @@ def tile_layernormlstmcell_kernel(
                     nc.scalar.activation(out=sq[:], in_=c_new[n][:], func=ACT.Square, bias=sm[:, 1:2], accum_out=sm[:, 2:3])
                 if t == cell_slot(n, C_TANH):
                     nc.scalar.activation(out=c_normed[n][:], in_=c_normed[n][:], func=ACT.Tanh)
+            for what, m, q in HEAD_SCALAR.get(t, ()):
+                if what == "interleave":
+                    w_interleave(m, q, nc.scalar.copy)
+                else:
+                    head["x"] = a_copy(turned["x"], nc.scalar.copy)
             period, place = divmod(t - CELL_LAG % 8, 8)
             if place == PREP_COPY and 2 <= period + 2 < TILES:
-                a_copy(period + 2)
-            if t == W_HH_COPY_SLOT_SCALAR:
-                w_interleave(1, 2, nc.scalar.copy)
+                grouped[period + 2] = a_copy(turned[period + 2], nc.scalar.copy)
             if t == GAIN_COPY_SLOT:
                 nc.scalar.copy(out=gain_cols[:], in_=spread_ps["gains"][:, 0:4 * GROUPS])
                 nc.gpsimd.tensor_tensor(
@@ -428,18 +532,19 @@ def tile_layernormlstmcell_kernel(
                     in1=gain_cols[:, 3 * GROUPS:4 * GROUPS],
                     op=ALU.add,
                 )
-                gamma_hh_cols = gain_cols[:, GROUPS:2 * GROUPS]
+                gamma_ih_cols = gain_cols[:, GROUPS:2 * GROUPS]
                 nc.gpsimd.tensor_scalar(
-                    out=near_zero[:], in0=gamma_hh_cols, scalar1=TINY, scalar2=2.0 * TINY, op0=ALU.is_lt, op1=ALU.mult
+                    out=near_zero[:], in0=gamma_ih_cols, scalar1=TINY, scalar2=2.0 * TINY, op0=ALU.is_lt, op1=ALU.mult
                 )
                 nc.gpsimd.tensor_scalar(
-                    out=divisor[:], in0=gamma_hh_cols, scalar1=-TINY, scalar2=1.0, op0=ALU.is_gt, op1=ALU.mult
+                    out=divisor[:], in0=gamma_ih_cols, scalar1=-TINY, scalar2=1.0, op0=ALU.is_gt, op1=ALU.mult
                 )
                 nc.gpsimd.tensor_tensor(out=near_zero[:], in0=near_zero[:], in1=divisor[:], op=ALU.mult)
-                nc.gpsimd.tensor_tensor(out=divisor[:], in0=gamma_hh_cols, in1=near_zero[:], op=ALU.add)
+                nc.gpsimd.tensor_tensor(out=divisor[:], in0=gamma_ih_cols, in1=near_zero[:], op=ALU.add)
+            if t == GAIN_COPY_SLOT + 2:
                 nc.vector.reciprocal(out=inverse[:], in_=divisor[:])
                 nc.gpsimd.tensor_tensor(out=ratio_cols[:], in0=gain_cols[:, 0:GROUPS], in1=inverse[:], op=ALU.mult)
-            elif t - 1 in RATIO_SPREAD_SLOTS:
+            if t - 1 in RATIO_SPREAD_SLOTS:
                 g = RATIO_SPREAD_SLOTS.index(t - 1)
                 nc.scalar.copy(out=ratio_all[:, g, :], in_=spread_ps[("ratio", g)][:].rearrange("p i c -> p (i c)"))
             elif t in CELL_GAIN_COPY_SLOTS:
@@ -449,9 +554,9 @@ def tile_layernormlstmcell_kernel(
         def turn_back(what, n, g, half):
             if half == 0:
                 if n >= TILES - 2:
-                    pool, tag = (ps_norm, "norm_acc") if what == "ig" else (ps_stat, "stat_acc")
+                    pool, tag = (ps_stat, "stat_acc") if what == "ig" else (ps_norm, "norm_acc")
                 else:
-                    pool, tag = ps_one, ("late" if what == "o" else "early")
+                    pool, tag = ps_one, ("late" if what == "o" and n != TILES - 3 else "early")
                 tl = pool.tile([P, H], F32, name=tag, tag=tag)
                 back_ps[(what, n)] = tl
             for jj in (2 * half, 2 * half + 1):
@@ -482,17 +587,29 @@ def tile_layernormlstmcell_kernel(
                     out=tl[:], lhsT=ones_bf16[:], rhs=cell_gain_row[:, which * H:(which + 1) * H], start=True, stop=True
                 )
                 spread_ps[which] = tl
+            if HEAD_TENSOR.get(t) == "x":
+                bank = turn_bank()
+                a_turn(bank, 0, 0, 1)
+                a_turn(bank, 1, 1, 1)
+                turned["x"] = bank
             for n in range(TILES):
                 for what, g, step in (("f", F_GATE, F_TURN), ("ig", I_GATE, IG_TURN), ("o", O_GATE, O_TURN)):
-                    if t - cell_slot(n, step) in (0, 1):
+                    if n < TILES - 4 and t - cell_slot(n, step) in (0, 1):
                         turn_back(what, n, g, t - cell_slot(n, step))
+                    elif n >= TILES - 4 and t == cell_slot(n, step):
+                        turn_back(what, n, g, 0)
+                        turn_back(what, n, g, 1)
             period, place = divmod(t - CELL_LAG % 8, 8)
             if place in (PREP_TURN, PREP_TURN + 1) and 2 <= period + 2 < TILES:
-                a_turn(period + 2, place - PREP_TURN)
-            u = t - TURN_LAG
-            if 0 <= u < UNITS:
+                n = period + 2
+                if place == PREP_TURN:
+                    turned[n] = turn_bank()
+                a_turn(turned[n], place - PREP_TURN, n, place - PREP_TURN)
+            for u in unit_at.get(t, ()):
                 pair, g, jj, j = unit_place(u)
-                tl = ps_unit.tile([P, 2, P], F32, name="unit_ps", tag="unit_ps")
+                spare = pair == PAIRS - 1 and g != O_GATE and jj % 2 == 1
+                pool, tag = (ps_stat, "stat_acc") if spare else (ps_unit, "unit_ps")
+                tl = pool.tile([P, 2, P], F32, name=tag, tag=tag)
                 for r in range(2):
                     for m in range(2):
                         nc.tensor.matmul(
@@ -507,12 +624,12 @@ def tile_layernormlstmcell_kernel(
 
         def product_slot(t):
             if t < PIECES:
-                n, m, q = stat_piece(t)
-                stat_acc[t] = product_piece(ps_stat, "stat_acc", n, m, q)
-            i = t - NORM_LAG
-            if 0 <= i < PIECES:
-                n, m, g = norm_piece(i)
-                norm_acc[i] = product_piece(ps_norm, "norm_acc", n, m, GATE_ORDER[g])
+                pair, m, q, r = stat_piece(t)
+                stat_acc[t] = product_piece(ps_stat, "stat_acc", 2 * pair + r, m, q)
+            for i in norm_at.get(t, ()):
+                pair, m, g, r = norm_piece(i)
+                pool, tag = (ps_stat, "stat_acc") if i >= PIECES - 8 and r == 1 else (ps_norm, "norm_acc")
+                norm_acc[i] = product_piece(pool, tag, 2 * pair + r, m, GATE_ORDER[g])
 
         for t in range(LAST_SLOT + 1):
             vector_slot(t)

@@ -45,7 +45,7 @@ LAST_IG_SLOTS = (4, 5)
 RATIO_LAG = 4
 PREP_WIDEN, PREP_TURN, PREP_COPY, PREP_QUANT = 3, 2, 4, 5
 GAIN_TURN_SLOT, GAIN_COPY_SLOT = 7, 8
-RATIO_SPREAD_SLOTS = (12, 14, 16, 18)
+RATIO_SPREAD_SLOTS = (13, 15, 17, 19)
 CELL_GAIN_SPREAD_SLOTS, CELL_GAIN_COPY_SLOTS = (20, 22), (21, 23)
 TINY = 2.0 ** -60
 Y_RING = (6, 7, 8, 8)
@@ -185,6 +185,8 @@ def tile_layernormlstmcell_kernel(
         nc.gpsimd.memset(ones_bf16[:], 1.0)
         neg_half = const.tile([P, 2], F32, name="neg_half", tag="neg_half")
         nc.gpsimd.memset(neg_half[:], -0.5)
+        eps_col = const.tile([P, 1], F32, name="eps_col", tag="eps_col")
+        nc.gpsimd.memset(eps_col[:], EPS)
         scale_all = const.tile([P, K], F32, name="scale_all", tag="scale_all")
         gamma_c_all = const.tile([P, H], BF16, name="gamma_c_all", tag="gamma_c_all")
         beta_c_all = const.tile([P, H], BF16, name="beta_c_all", tag="beta_c_all")
@@ -371,12 +373,6 @@ def tile_layernormlstmcell_kernel(
                         out=tl[:], in0=norm_acc[i][:], scalar1=fac[:, r:r + 1], scalar2=fac[:, 2 + r:3 + r], op0=ALU.mult, op1=ALU.add
                     )
                     y[(pair, g, r, m)] = tl
-            e = t - 4
-            if 0 <= e < PIECES and e % 8 == 7:
-                k = stat_piece(e)[0:2]
-                nc.vector.scalar_tensor_tensor(
-                    out=factors[k][:, 2:4], in0=moments[k][:, 0:4:2], scalar=-1.0, in1=factors[k][:, 0:2], op0=ALU.mult, op1=ALU.mult
-                )
             e = t - 1
             if 0 <= e < PIECES and e % 8 == 7:
                 k = stat_piece(e)[0:2]
@@ -422,13 +418,11 @@ def tile_layernormlstmcell_kernel(
                     tl = cell.tile([P, H], F32, name="h_new", tag="h_new")
                     nc.vector.tensor_tensor(out=tl[:], in0=back_ps[("o", n)][:], in1=c_normed[n][:], op=ALU.mult)
                     nc.sync.dma_start(out=out_0[rows, :], in_=tl[:])
-            e = t - 1
+            e = t - 2
             if 0 <= e < PIECES and e % 8 == 7:
                 k = stat_piece(e)[0:2]
-                nc.vector.tensor_scalar(
-                    out=moments[k][:, 4:6], in0=moments[k][:, 1:4:2], scalar1=1.0, scalar2=EPS, op0=ALU.mult, op1=ALU.add
-                )
                 nc.gpsimd.tensor_tensor(out=factors[k][:, 0:2], in0=moments[k][:, 4:6], in1=neg_half[:], op=ALU.pow)
+                nc.gpsimd.tensor_tensor(out=factors[k][:, 2:4], in0=moments[k][:, 6:8], in1=factors[k][:, 0:2], op=ALU.mult)
             for pair, g, r in ratio_at.get(t, ()):
                 if not ratio_on_vector(pair, g, r):
                     v = y[(pair, g, r, 0)][:]
@@ -503,12 +497,8 @@ def tile_layernormlstmcell_kernel(
                     y[(pair, g, r, m)] = tl
 
         def scalar_slot(t):
-            if t % 2 == 0:
-                normalise(t)
-                finish_gate(t)
-            else:
-                finish_gate(t)
-                normalise(t)
+            normalise(t)
+            finish_gate(t)
             for n in range(TILES):
                 if t == cell_slot(n, C_SQUARE):
                     sm = c_small[n]
@@ -516,6 +506,11 @@ def tile_layernormlstmcell_kernel(
                     nc.scalar.activation(out=sq[:], in_=c_new[n][:], func=ACT.Square, bias=sm[:, 1:2], accum_out=sm[:, 2:3])
                 if t == cell_slot(n, C_TANH):
                     nc.scalar.activation(out=c_normed[n][:], in_=c_normed[n][:], func=ACT.Tanh)
+            e = t - 1
+            if 0 <= e < PIECES and e % 8 == 7:
+                k = stat_piece(e)[0:2]
+                nc.scalar.activation(out=moments[k][:, 4:6], in_=moments[k][:, 1:4:2], func=ACT.Identity, bias=eps_col[:])
+                nc.scalar.activation(out=moments[k][:, 6:8], in_=moments[k][:, 0:4:2], func=ACT.Identity, scale=-1.0)
             for what, m, q in HEAD_SCALAR.get(t, ()):
                 if what == "interleave":
                     w_interleave(m, q, nc.scalar.copy)
@@ -541,7 +536,7 @@ def tile_layernormlstmcell_kernel(
                 )
                 nc.gpsimd.tensor_tensor(out=near_zero[:], in0=near_zero[:], in1=divisor[:], op=ALU.mult)
                 nc.gpsimd.tensor_tensor(out=divisor[:], in0=gamma_ih_cols, in1=near_zero[:], op=ALU.add)
-            if t == GAIN_COPY_SLOT + 2:
+            if t == GAIN_COPY_SLOT + 4:
                 nc.vector.reciprocal(out=inverse[:], in_=divisor[:])
                 nc.gpsimd.tensor_tensor(out=ratio_cols[:], in0=gain_cols[:, 0:GROUPS], in1=inverse[:], op=ALU.mult)
             if t - 1 in RATIO_SPREAD_SLOTS:
@@ -576,9 +571,7 @@ def tile_layernormlstmcell_kernel(
                 tl = ps_unit.tile([P, 4, P], F32, name="unit_ps", tag="unit_ps")
                 for jj in range(4):
                     j = 4 * GATE_ORDER[g] + jj
-                    nc.tensor.matmul(
-                        out=tl[:, jj, :], lhsT=ratio_cols[:, j:j + 1].to_broadcast([P, P]), rhs=ident[:], start=True, stop=True
-                    )
+                    nc.tensor.transpose(tl[:, jj, :], ratio_cols[:, j:j + 1].to_broadcast([P, P]), ident[:])
                 spread_ps[("ratio", g)] = tl
             elif t in CELL_GAIN_SPREAD_SLOTS:
                 which = CELL_GAIN_SPREAD_SLOTS.index(t)
@@ -592,19 +585,6 @@ def tile_layernormlstmcell_kernel(
                 a_turn(bank, 0, 0, 1)
                 a_turn(bank, 1, 1, 1)
                 turned["x"] = bank
-            for n in range(TILES):
-                for what, g, step in (("f", F_GATE, F_TURN), ("ig", I_GATE, IG_TURN), ("o", O_GATE, O_TURN)):
-                    if n < TILES - 4 and t - cell_slot(n, step) in (0, 1):
-                        turn_back(what, n, g, t - cell_slot(n, step))
-                    elif n >= TILES - 4 and t == cell_slot(n, step):
-                        turn_back(what, n, g, 0)
-                        turn_back(what, n, g, 1)
-            period, place = divmod(t - CELL_LAG % 8, 8)
-            if place in (PREP_TURN, PREP_TURN + 1) and 2 <= period + 2 < TILES:
-                n = period + 2
-                if place == PREP_TURN:
-                    turned[n] = turn_bank()
-                a_turn(turned[n], place - PREP_TURN, n, place - PREP_TURN)
             for u in unit_at.get(t, ()):
                 pair, g, jj, j = unit_place(u)
                 spare = pair == PAIRS - 1 and g != O_GATE and jj % 2 == 1
@@ -621,6 +601,19 @@ def tile_layernormlstmcell_kernel(
                             stop=(m == 1),
                         )
                 unit_ps[u] = tl
+            for n in range(TILES):
+                for what, g, step in (("f", F_GATE, F_TURN), ("ig", I_GATE, IG_TURN), ("o", O_GATE, O_TURN)):
+                    if n < TILES - 4 and t - cell_slot(n, step) in (0, 1):
+                        turn_back(what, n, g, t - cell_slot(n, step))
+                    elif n >= TILES - 4 and t == cell_slot(n, step):
+                        turn_back(what, n, g, 0)
+                        turn_back(what, n, g, 1)
+            period, place = divmod(t - CELL_LAG % 8, 8)
+            if place in (PREP_TURN, PREP_TURN + 1) and 2 <= period + 2 < TILES:
+                n = period + 2
+                if place == PREP_TURN:
+                    turned[n] = turn_bank()
+                a_turn(turned[n], place - PREP_TURN, n, place - PREP_TURN)
 
         def product_slot(t):
             if t < PIECES:
@@ -634,9 +627,5 @@ def tile_layernormlstmcell_kernel(
         for t in range(LAST_SLOT + 1):
             vector_slot(t)
             scalar_slot(t)
-            if t % 2 == 0:
-                turn_slot(t)
-                product_slot(t)
-            else:
-                product_slot(t)
-                turn_slot(t)
+            product_slot(t)
+            turn_slot(t)

@@ -33,20 +33,20 @@ NORM_LAG = 11
 TURN_LAG = NORM_LAG + 11
 CELL_LAG = TURN_LAG + 13
 F_TURN, F_C, IG_TURN, C_SUM, C_SQUARE, C_GAIN, C_SHIFT, C_TANH, O_TURN, H_OUT = 0, 1, 2, 3, 4, 5, 6, 7, 8, 9
-CELL_STEPS = (0, 2, 4, 6, 7, 9, 12, 14, 14, 16)
+CELL_STEPS = (0, 1, 4, 5, 7, 8, 12, 13, 14, 15)
 LAST_CELL_STEPS = (0, 1, 1, 2, 3, 4, 6, 7, 3, 8)
 MID_CELL_SLOT = CELL_LAG + 8 * (TILES - 4) - 0
-MID_CELL_STEPS = (0, 1, 2, 3, 4, 5, 7, 8, 8, 10)
+MID_CELL_STEPS = (0, 1, 2, 3, 4, 5, 7, 8, 8, 9)
 LAST_NORM_SLOT = 131
 LAST_UNIT_SLOT = LAST_NORM_SLOT + 2
 LAST_CELL_SLOT = LAST_UNIT_SLOT + 6
 IG_SLOTS = (8, 13)
 LAST_IG_SLOTS = (4, 5)
 RATIO_LAG = 4
-PREP_WIDEN, PREP_TURN, PREP_COPY, PREP_QUANT = 3, 2, 4, 5
+PREP_WIDEN, PREP_TURN, PREP_COPY, PREP_QUANT = 6, 2, 3, 4
 GAIN_TURN_SLOT, GAIN_COPY_SLOT = 7, 8
 RATIO_SPREAD_SLOTS = (13, 15, 17, 19)
-CELL_GAIN_SPREAD_SLOTS, CELL_GAIN_COPY_SLOTS = (20, 22), (21, 23)
+CELL_GAIN_SPREAD_SLOTS = (20, 21)
 TINY = 2.0 ** -60
 Y_RING = (6, 7, 8, 8)
 
@@ -117,7 +117,8 @@ def tile_layernormlstmcell_kernel(
         ps_stat = ctx.enter_context(tc.psum_pool(name="ps_stat", bufs=2))
         ps_norm = ctx.enter_context(tc.psum_pool(name="ps_norm", bufs=2))
         ps_unit = ctx.enter_context(tc.psum_pool(name="ps_unit", bufs=2))
-        ps_one = ctx.enter_context(tc.psum_pool(name="ps_one", bufs=1))
+        ps_back = ctx.enter_context(tc.psum_pool(name="ps_back", bufs=1))
+        ps_gain = ctx.enter_context(tc.psum_pool(name="ps_gain", bufs=1))
         ctx.enter_context(tc.manual_schedule())
 
         w_views = (
@@ -188,8 +189,7 @@ def tile_layernormlstmcell_kernel(
         eps_col = const.tile([P, 1], F32, name="eps_col", tag="eps_col")
         nc.gpsimd.memset(eps_col[:], EPS)
         scale_all = const.tile([P, K], F32, name="scale_all", tag="scale_all")
-        gamma_c_all = const.tile([P, H], BF16, name="gamma_c_all", tag="gamma_c_all")
-        beta_c_all = const.tile([P, H], BF16, name="beta_c_all", tag="beta_c_all")
+        cell_gains = ps_gain.tile([P, 2, H], BF16, name="cell_gains", tag="cell_gains")
         gain_cols = const.tile([P, 4 * GROUPS], F32, name="gain_cols", tag="gain_cols")
         beta_cols = const.tile([P, GROUPS], F32, name="beta_cols", tag="beta_cols")
         near_zero = const.tile([P, GROUPS], F32, name="near_zero", tag="near_zero")
@@ -237,7 +237,7 @@ def tile_layernormlstmcell_kernel(
                 nc.tensor.transpose(bank[:, 2 * place + u, :], words[:, u:K // 2:2], ident[:])
 
         def turn_bank():
-            t = ps_one.tile([P, 2 * 2, P], F32, name="late", tag="late")
+            t = ps_back.tile([P, 2 * 2, P], F32, name="back", tag="back")
             return t
 
         def a_copy(bank, copy):
@@ -406,13 +406,13 @@ def tile_layernormlstmcell_kernel(
                 if t == cell_slot(n, C_GAIN):
                     tl = cell.tile([P, H], F32, name="c_normed", tag="c_normed")
                     nc.vector.scalar_tensor_tensor(
-                        out=tl[:], in0=c_new[n][:], scalar=c_small[n][:, 1:2], in1=gamma_c_all[:], op0=ALU.add, op1=ALU.mult
+                        out=tl[:], in0=c_new[n][:], scalar=c_small[n][:, 1:2], in1=cell_gains[:, 0, :], op0=ALU.add, op1=ALU.mult
                     )
                     c_normed[n] = tl
                 elif t == cell_slot(n, C_SHIFT):
                     v = c_normed[n][:]
                     nc.vector.scalar_tensor_tensor(
-                        out=v, in0=v, scalar=c_small[n][:, 4:5], in1=beta_c_all[:], op0=ALU.mult, op1=ALU.add
+                        out=v, in0=v, scalar=c_small[n][:, 4:5], in1=cell_gains[:, 1, :], op0=ALU.mult, op1=ALU.add
                     )
                 elif t == cell_slot(n, H_OUT):
                     tl = cell.tile([P, H], F32, name="h_new", tag="h_new")
@@ -497,8 +497,12 @@ def tile_layernormlstmcell_kernel(
                     y[(pair, g, r, m)] = tl
 
         def scalar_slot(t):
-            normalise(t)
-            finish_gate(t)
+            if t % 2 in (0,):
+                normalise(t)
+                finish_gate(t)
+            else:
+                finish_gate(t)
+                normalise(t)
             for n in range(TILES):
                 if t == cell_slot(n, C_SQUARE):
                     sm = c_small[n]
@@ -542,16 +546,13 @@ def tile_layernormlstmcell_kernel(
             if t - 1 in RATIO_SPREAD_SLOTS:
                 g = RATIO_SPREAD_SLOTS.index(t - 1)
                 nc.scalar.copy(out=ratio_all[:, g, :], in_=spread_ps[("ratio", g)][:].rearrange("p i c -> p (i c)"))
-            elif t in CELL_GAIN_COPY_SLOTS:
-                which = CELL_GAIN_COPY_SLOTS.index(t)
-                nc.scalar.copy(out=(gamma_c_all, beta_c_all)[which][:], in_=spread_ps[which][:])
 
         def turn_back(what, n, g, half):
             if half == 0:
                 if n >= TILES - 2:
                     pool, tag = (ps_stat, "stat_acc") if what == "ig" else (ps_norm, "norm_acc")
                 else:
-                    pool, tag = ps_one, ("late" if what == "o" and n != TILES - 3 else "early")
+                    pool, tag = ps_back, "back"
                 tl = pool.tile([P, H], F32, name=tag, tag=tag)
                 back_ps[(what, n)] = tl
             for jj in (2 * half, 2 * half + 1):
@@ -563,7 +564,7 @@ def tile_layernormlstmcell_kernel(
 
         def turn_slot(t):
             if t == GAIN_TURN_SLOT:
-                tl = ps_one.tile([P, P], BF16, name="early", tag="early")
+                tl = ps_unit.tile([P, P], BF16, name="unit_ps", tag="unit_ps")
                 nc.tensor.transpose(tl[:], gain_rows[:], ident_bf16[:])
                 spread_ps["gains"] = tl
             elif t in RATIO_SPREAD_SLOTS:
@@ -575,11 +576,9 @@ def tile_layernormlstmcell_kernel(
                 spread_ps[("ratio", g)] = tl
             elif t in CELL_GAIN_SPREAD_SLOTS:
                 which = CELL_GAIN_SPREAD_SLOTS.index(t)
-                tl = ps_one.tile([P, H], F32, name="early", tag="early")
                 nc.tensor.matmul(
-                    out=tl[:], lhsT=ones_bf16[:], rhs=cell_gain_row[:, which * H:(which + 1) * H], start=True, stop=True
+                    out=cell_gains[:, which, :], lhsT=ones_bf16[:], rhs=cell_gain_row[:, which * H:(which + 1) * H], start=True, stop=True
                 )
-                spread_ps[which] = tl
             if HEAD_TENSOR.get(t) == "x":
                 bank = turn_bank()
                 a_turn(bank, 0, 0, 1)
@@ -603,17 +602,15 @@ def tile_layernormlstmcell_kernel(
                 unit_ps[u] = tl
             for n in range(TILES):
                 for what, g, step in (("f", F_GATE, F_TURN), ("ig", I_GATE, IG_TURN), ("o", O_GATE, O_TURN)):
-                    if n < TILES - 4 and t - cell_slot(n, step) in (0, 1):
-                        turn_back(what, n, g, t - cell_slot(n, step))
-                    elif n >= TILES - 4 and t == cell_slot(n, step):
+                    if t == cell_slot(n, step):
                         turn_back(what, n, g, 0)
                         turn_back(what, n, g, 1)
             period, place = divmod(t - CELL_LAG % 8, 8)
-            if place in (PREP_TURN, PREP_TURN + 1) and 2 <= period + 2 < TILES:
+            if place == PREP_TURN and 2 <= period + 2 < TILES:
                 n = period + 2
-                if place == PREP_TURN:
-                    turned[n] = turn_bank()
-                a_turn(turned[n], place - PREP_TURN, n, place - PREP_TURN)
+                turned[n] = turn_bank()
+                for m in range(2):
+                    a_turn(turned[n], m, n, m)
 
         def product_slot(t):
             if t < PIECES:
@@ -627,5 +624,9 @@ def tile_layernormlstmcell_kernel(
         for t in range(LAST_SLOT + 1):
             vector_slot(t)
             scalar_slot(t)
-            product_slot(t)
-            turn_slot(t)
+            if t % 2 in (1,):
+                product_slot(t)
+                turn_slot(t)
+            else:
+                turn_slot(t)
+                product_slot(t)

@@ -33,18 +33,18 @@ NORM_LAG = 11
 TURN_LAG = NORM_LAG + 11
 CELL_LAG = TURN_LAG + 13
 F_TURN, F_C, IG_TURN, C_SUM, C_SQUARE, C_GAIN, C_SHIFT, C_TANH, O_TURN, H_OUT = 0, 1, 2, 3, 4, 5, 6, 7, 8, 9
-CELL_STEPS = (0, 1, 4, 5, 7, 8, 12, 13, 14, 15)
+CELL_STEPS = (0, 1, 4, 5, 7, 8, 11, 12, 14, 15)
 LAST_CELL_STEPS = (0, 1, 1, 2, 3, 4, 6, 7, 3, 8)
 MID_CELL_SLOT = CELL_LAG + 8 * (TILES - 4) - 0
 MID_CELL_STEPS = (0, 1, 2, 3, 4, 5, 7, 8, 8, 9)
 LAST_NORM_SLOT = 131
 LAST_UNIT_SLOT = LAST_NORM_SLOT + 2
-LAST_CELL_SLOT = LAST_UNIT_SLOT + 6
+LAST_CELL_SLOT = LAST_UNIT_SLOT + 7
 IG_SLOTS = (8, 13)
 LAST_IG_SLOTS = (4, 5)
 RATIO_LAG = 4
-PREP_WIDEN, PREP_TURN, PREP_COPY, PREP_QUANT = 6, 2, 3, 4
-GAIN_TURN_SLOT, GAIN_COPY_SLOT = 7, 8
+PREP_WIDEN, PREP_TURN, PREP_COPY, PREP_QUANT = 7, 2, 3, 4
+GAIN_TURN_SLOT, GAIN_COPY_SLOT = 6, 7
 RATIO_SPREAD_SLOTS = (13, 15, 17, 19)
 CELL_GAIN_SPREAD_SLOTS = (20, 21)
 TINY = 2.0 ** -60
@@ -329,7 +329,7 @@ def tile_layernormlstmcell_kernel(
             return tl
 
         def ratio_on_vector(pair, g, r):
-            return r == 1 and pair == PAIRS - 1
+            return g > 1 and pair == PAIRS - 1
 
         def norm_on_vector(pair, m, g, r):
             return pair == PAIRS - 1 and m == 1 and r == 1
@@ -429,7 +429,8 @@ def tile_layernormlstmcell_kernel(
                     nc.gpsimd.tensor_tensor(out=v, in0=v, in1=ratio_all[:, g, :], op=ALU.mult)
             for pair, half in ig_at.get(t, ()):
                 iv = half_gate(pair, I_GATE, half)
-                nc.gpsimd.tensor_tensor(out=iv, in0=iv, in1=half_gate(pair, G_GATE, half), op=ALU.mult)
+                engine = nc.gpsimd if pair < PAIRS - 1 else nc.vector
+                engine.tensor_tensor(out=iv, in0=iv, in1=half_gate(pair, G_GATE, half), op=ALU.mult)
             for what, m, q in HEAD_VECTOR.get(t, ()):
                 if what == "interleave":
                     w_interleave(m, q, nc.vector.tensor_copy)
@@ -440,8 +441,10 @@ def tile_layernormlstmcell_kernel(
                 else:
                     a_quantize(head["x"], ((0, 1), (1, 1)))
             period, place = divmod(t - CELL_LAG % 8, 8)
-            if place == PREP_WIDEN and 2 <= period + 3 < TILES:
+            if place == PREP_WIDEN and 3 <= period + 3 < TILES:
                 a_widen(period + 3)
+            if place == PREP_COPY and 2 <= period + 2 < TILES:
+                grouped[period + 2] = a_copy(turned[period + 2], nc.vector.tensor_copy)
             if place == PREP_QUANT and 2 <= period + 2 < TILES:
                 n = period + 2
                 a_quantize(grouped[n], ((n, 0), (n, 1)))
@@ -521,8 +524,6 @@ def tile_layernormlstmcell_kernel(
                 else:
                     head["x"] = a_copy(turned["x"], nc.scalar.copy)
             period, place = divmod(t - CELL_LAG % 8, 8)
-            if place == PREP_COPY and 2 <= period + 2 < TILES:
-                grouped[period + 2] = a_copy(turned[period + 2], nc.scalar.copy)
             if t == GAIN_COPY_SLOT:
                 nc.scalar.copy(out=gain_cols[:], in_=spread_ps["gains"][:, 0:4 * GROUPS])
                 nc.gpsimd.tensor_tensor(
@@ -589,6 +590,11 @@ def tile_layernormlstmcell_kernel(
                 spare = pair == PAIRS - 1 and g != O_GATE and jj % 2 == 1
                 pool, tag = (ps_stat, "stat_acc") if spare else (ps_unit, "unit_ps")
                 tl = pool.tile([P, 2, P], F32, name=tag, tag=tag)
+                if pair == PAIRS - 1:
+                    for i in range(2 - jj % 2):
+                        nc.tensor.matmul(
+                            out=tl[:].rearrange("p r t -> p (r t)"), lhsT=ones_bf16[:], rhs=cell_gain_row[:, 0:2 * P], start=True, stop=True
+                        )
                 for r in range(2):
                     for m in range(2):
                         nc.tensor.matmul(

@@ -146,7 +146,7 @@ def tile_layernormlstmcell_kernel(
         def load_h(lo, hi):
             nc.sync.dma_start(out=h_sb[:, lo:hi, :], in_=h_view[:, lo:hi, :])
 
-        scale_row = const.tile([P, K], F32, name="scale_row", tag="scale_row")
+        scale_cols = const.tile([P, PACK], F32, name="scale_cols", tag="scale_cols")
         cell_gain_row = const.tile([P, 2 * H], BF16, name="cell_gain_row", tag="cell_gain_row")
         gain_rows = const.tile([P, P], BF16, name="gain_rows", tag="gain_rows")
         ident = const.tile([P, P], F32, name="ident", tag="ident")
@@ -155,8 +155,7 @@ def tile_layernormlstmcell_kernel(
         load_w(0, 0, 1)
         load_w(0, 1, 2)
         make_identity(nc, ident[:])
-        nc.gpsimd.memset(scale_row[:], 0.0)
-        nc.sync.dma_start(out=scale_row[0:1, :], in_=x_scale)
+        nc.sync.dma_start(out=scale_cols[:], in_=x_scale.rearrange("o (p j) -> p (o j)", j=PACK))
         load_x(0, 2)
         load_w(0, 2, 4)
         nc.vector.memset(gain_rows[:], 0.0)
@@ -175,8 +174,6 @@ def tile_layernormlstmcell_kernel(
         for lo in (0, 4, 8, 12):
             nc.sync.dma_start(out=c_sb[:, lo:lo + 4, :], in_=c_view[:, lo:lo + 4, :])
 
-        ones_f32 = const.tile([P, P], F32, name="ones_f32", tag="ones_f32")
-        nc.gpsimd.memset(ones_f32[:], 1.0)
         warm = const.tile([P, 1], F32, name="warm", tag="warm")
         nc.gpsimd.memset(warm[:], 0.0)
         nc.scalar.activation(out=warm[:], in_=warm[:], func=ACT.Sigmoid)
@@ -275,10 +272,11 @@ def tile_layernormlstmcell_kernel(
         h_bank = turn_bank()
         a_turn(h_bank, 0, 0, 0)
         a_turn(h_bank, 1, 1, 0)
-        scale_ps = ps_unit.tile([P, K], F32, name="unit_ps", tag="unit_ps")
-        nc.tensor.matmul(out=scale_ps[:], lhsT=ones_f32[:], rhs=scale_row[:], start=True, stop=True)
+        scale_ps = ps_unit.tile([P, PACK, P], F32, name="unit_ps", tag="unit_ps")
+        for j in range(PACK):
+            nc.tensor.transpose(scale_ps[:, j, :], scale_cols[:, j:j + 1].to_broadcast([P, P]), ident[:])
         head["h"] = a_copy(h_bank, nc.scalar.copy)
-        nc.scalar.copy(out=scale_all[:], in_=scale_ps[:])
+        nc.scalar.copy(out=scale_all[:].rearrange("p (q j) -> p q j", j=PACK), in_=scale_ps[:].rearrange("p j q -> p q j"))
         w_interleave(0, 0, nc.vector.tensor_copy)
         a_quantize(head["h"], ((0, 0), (1, 0)))
         w_quantize(0, 0)
@@ -429,8 +427,7 @@ def tile_layernormlstmcell_kernel(
                     nc.gpsimd.tensor_tensor(out=v, in0=v, in1=ratio_all[:, g, :], op=ALU.mult)
             for pair, half in ig_at.get(t, ()):
                 iv = half_gate(pair, I_GATE, half)
-                engine = nc.gpsimd if pair < PAIRS - 1 else nc.vector
-                engine.tensor_tensor(out=iv, in0=iv, in1=half_gate(pair, G_GATE, half), op=ALU.mult)
+                nc.gpsimd.tensor_tensor(out=iv, in0=iv, in1=half_gate(pair, G_GATE, half), op=ALU.mult)
             for what, m, q in HEAD_VECTOR.get(t, ()):
                 if what == "interleave":
                     w_interleave(m, q, nc.vector.tensor_copy)
@@ -590,11 +587,6 @@ def tile_layernormlstmcell_kernel(
                 spare = pair == PAIRS - 1 and g != O_GATE and jj % 2 == 1
                 pool, tag = (ps_stat, "stat_acc") if spare else (ps_unit, "unit_ps")
                 tl = pool.tile([P, 2, P], F32, name=tag, tag=tag)
-                if pair == PAIRS - 1:
-                    for i in range(2 - jj % 2):
-                        nc.tensor.matmul(
-                            out=tl[:].rearrange("p r t -> p (r t)"), lhsT=ones_bf16[:], rhs=cell_gain_row[:, 0:2 * P], start=True, stop=True
-                        )
                 for r in range(2):
                     for m in range(2):
                         nc.tensor.matmul(

@@ -42,7 +42,7 @@ LAST_UNIT_SLOT = LAST_NORM_SLOT + 2
 LAST_CELL_SLOT = LAST_UNIT_SLOT + 7
 IG_SLOTS = (8, 13)
 LAST_IG_SLOTS = (4, 5)
-RATIO_LAG = 4
+RATIO_LAG = 6
 PREP_WIDEN, PREP_TURN, PREP_COPY, PREP_QUANT = 7, 2, 3, 4
 GAIN_TURN_SLOT, GAIN_COPY_SLOT = 6, 7
 RATIO_SPREAD_SLOTS = (13, 15, 17, 19)

@@ -43,7 +43,7 @@ LAST_CELL_SLOT = LAST_UNIT_SLOT + 7
 IG_SLOTS = (8, 13)
 LAST_IG_SLOTS = (4, 5)
 RATIO_LAG = 6
-PREP_WIDEN, PREP_TURN, PREP_COPY, PREP_QUANT = 7, 2, 3, 4
+PREP_WIDEN, PREP_TURN, PREP_COPY, PREP_QUANT = 6, 2, 3, 4
 GAIN_TURN_SLOT, GAIN_COPY_SLOT = 6, 7
 RATIO_SPREAD_SLOTS = (13, 15, 17, 19)
 CELL_GAIN_SPREAD_SLOTS = (20, 21)

from contextlib import ExitStack

import concourse.mybir as mybir
from concourse.masks import make_identity

F32 = mybir.dt.float32
BF16 = mybir.dt.bfloat16
U32 = mybir.dt.uint32
U8 = mybir.dt.uint8
FP8 = mybir.dt.float8_e4m3fn
FP8X4 = mybir.dt.float8_e4m3fn_x4
ALU = mybir.AluOpType
ACT = mybir.ActivationFunctionType

TOKENS, K, H, GATES = 2048, 512, 512, 2048
EPS = 1e-5
FLOPS = 2 * 2 * TOKENS * K * GATES

P = 128
PACK = 4
BANK = 512
CHUNK_BYTES = PACK * BANK * 2
TILES = TOKENS // P
PAIRS = TILES // 2
PIECES = 8 * TILES
GROUPS = GATES // P
UNITS = GROUPS * PAIRS
STATS_DIM = 6
GATE_ORDER = (0, 2, 1, 3)
I_GATE, G_GATE, F_GATE, O_GATE = 0, 1, 2, 3

NORM_LAG = 11
TURN_LAG = NORM_LAG + 11
CELL_LAG = TURN_LAG + 13
F_TURN, F_C, IG_TURN, C_SUM, C_SQUARE, C_GAIN, C_SHIFT, C_TANH, O_TURN, H_OUT = 0, 1, 2, 3, 4, 5, 6, 7, 8, 9
CELL_STEPS = (0, 1, 4, 5, 7, 8, 11, 12, 14, 15)
LAST_CELL_STEPS = (0, 1, 1, 2, 3, 4, 6, 7, 3, 8)
MID_CELL_SLOT = CELL_LAG + 8 * (TILES - 4) - 0
MID_CELL_STEPS = (0, 1, 2, 3, 4, 5, 7, 8, 8, 9)
LAST_NORM_SLOT = 131
LAST_UNIT_SLOT = LAST_NORM_SLOT + 2
LAST_CELL_SLOT = LAST_UNIT_SLOT + 7
IG_SLOTS = (8, 13)
LAST_IG_SLOTS = (4, 5)
RATIO_LAG = 6
PREP_WIDEN, PREP_TURN, PREP_COPY, PREP_QUANT = 6, 2, 3, 4
GAIN_TURN_SLOT, GAIN_COPY_SLOT = 6, 7
RATIO_SPREAD_SLOTS = (13, 15, 17, 19)
CELL_GAIN_SPREAD_SLOTS = (20, 21)
TINY = 2.0 ** -60
Y_RING = (6, 7, 8, 8)


def norm_slot(i):
    if i < PIECES - 8:
        return i + NORM_LAG
    return LAST_NORM_SLOT + (i - (PIECES - 8)) // 4


def unit_slot(u):
    if u < UNITS - GROUPS:
        return u + TURN_LAG
    return LAST_UNIT_SLOT + (u - (UNITS - GROUPS)) // 2


def ratio_slot(pair, k):
    return 16 * pair + NORM_LAG + RATIO_LAG + (2 * k if pair < PAIRS - 1 else k)


def ig_slot(pair, half):
    if pair < PAIRS - 1:
        return 16 * pair + TURN_LAG + IG_SLOTS[half]
    return LAST_UNIT_SLOT + LAST_IG_SLOTS[half]


def cell_start(n):
    if n < TILES - 4:
        return CELL_LAG + 8 * n
    if n < TILES - 2:
        return MID_CELL_SLOT + n % 2
    return LAST_CELL_SLOT


def cell_slot(n, step):
    steps = CELL_STEPS if n < TILES - 4 else MID_CELL_STEPS if n < TILES - 2 else LAST_CELL_STEPS
    return cell_start(n) + steps[step]


LAST_SLOT = max(cell_slot(n, H_OUT) for n in range(TILES))


def tile_layernormlstmcell_kernel(
    tc,
    x_bytes,
    x_scale,
    h_prev,
    c_prev,
    W_ih,
    W_hh,
    gamma_ih,
    beta_ih,
    gamma_hh,
    beta_hh,
    gamma_c,
    beta_c,
    out_0,
    out_1,
):
    nc = tc.nc
    with ExitStack() as ctx:
        const = ctx.enter_context(tc.tile_pool(name="const", bufs=1))
        stage = ctx.enter_context(tc.tile_pool(name="stage", bufs=1))
        prep = ctx.enter_context(tc.tile_pool(name="prep", bufs=2))
        gates = ctx.enter_context(tc.tile_pool(name="gates", bufs=2))
        cell = ctx.enter_context(tc.tile_pool(name="cell", bufs=3))
        small = ctx.enter_context(tc.tile_pool(name="small", bufs=3))
        ps_stat = ctx.enter_context(tc.psum_pool(name="ps_stat", bufs=2))
        ps_norm = ctx.enter_context(tc.psum_pool(name="ps_norm", bufs=2))
        ps_unit = ctx.enter_context(tc.psum_pool(name="ps_unit", bufs=2))
        ps_back = ctx.enter_context(tc.psum_pool(name="ps_back", bufs=1))
        ps_gain = ctx.enter_context(tc.psum_pool(name="ps_gain", bufs=1))
        ctx.enter_context(tc.manual_schedule())

        w_views = (
            W_hh.rearrange("(p j) w -> p j w", j=PACK),
            W_ih.rearrange("(p j) w -> p j w", j=PACK),
        )
        w_raw = {}

        def load_w(m, q_lo, q_hi):
            t = stage.tile([P, PACK, (q_hi - q_lo) * BANK], BF16, name="w_raw_%d_%d" % (m, q_lo), offset=(4 * m + q_lo) * CHUNK_BYTES)
            nc.sync.dma_start(out=t[:], in_=w_views[m][:, :, q_lo * BANK:q_hi * BANK])
            for q in range(q_lo, q_hi):
                w_raw[(m, q)] = t[:, :, (q - q_lo) * BANK:(q - q_lo + 1) * BANK]

        x_sb = const.tile([P, TILES, K], U8, name="x_sb", tag="x_sb")
        h_sb = const.tile([P, TILES, K], BF16, name="h_sb", tag="h_sb")
        c_sb = const.tile([P, TILES, H], BF16, name="c_sb", tag="c_sb")
        x_view = x_bytes.rearrange("(n p) k -> p n k", p=P)
        h_view = h_prev.rearrange("(n p) k -> p n k", p=P)
        c_view = c_prev.rearrange("(n p) k -> p n k", p=P)

        def load_x(lo, hi):
            nc.sync.dma_start(out=x_sb[:, lo:hi, :], in_=x_view[:, lo:hi, :])

        def load_h(lo, hi):
            nc.sync.dma_start(out=h_sb[:, lo:hi, :], in_=h_view[:, lo:hi, :])

        scale_cols = const.tile([P, PACK], F32, name="scale_cols", tag="scale_cols")
        cell_gain_row = const.tile([P, 2 * H], BF16, name="cell_gain_row", tag="cell_gain_row")
        gain_rows = const.tile([P, P], BF16, name="gain_rows", tag="gain_rows")
        ident = const.tile([P, P], F32, name="ident", tag="ident")

        load_h(0, 2)
        load_w(0, 0, 1)
        load_w(0, 1, 2)
        make_identity(nc, ident[:])
        nc.sync.dma_start(out=scale_cols[:], in_=x_scale.rearrange("o (p j) -> p (o j)", j=PACK))
        load_x(0, 2)
        load_w(0, 2, 4)
        nc.vector.memset(gain_rows[:], 0.0)
        for i, vec in enumerate((gamma_hh, gamma_ih, beta_hh, beta_ih)):
            nc.sync.dma_start(out=gain_rows[GROUPS * i:GROUPS * (i + 1), :], in_=vec.rearrange("(j p) -> j p", p=P))
        load_h(2, 4)
        load_x(2, 4)
        load_w(1, 0, 2)
        load_w(1, 2, 4)
        nc.gpsimd.memset(cell_gain_row[:], 0.0)
        nc.sync.dma_start(out=cell_gain_row[0:1, 0:H], in_=gamma_c.rearrange("(o k) -> o k", o=1))
        nc.sync.dma_start(out=cell_gain_row[0:1, H:2 * H], in_=beta_c.rearrange("(o k) -> o k", o=1))
        for lo in (4, 8, 12):
            load_h(lo, lo + 4)
            load_x(lo, lo + 4)
        for lo in (0, 4, 8, 12):
            nc.sync.dma_start(out=c_sb[:, lo:lo + 4, :], in_=c_view[:, lo:lo + 4, :])

        warm = const.tile([P, 1], F32, name="warm", tag="warm")
        nc.gpsimd.memset(warm[:], 0.0)
        nc.scalar.activation(out=warm[:], in_=warm[:], func=ACT.Sigmoid)
        ident_bf16 = const.tile([P, P], BF16, name="ident_bf16", tag="ident_bf16")
        make_identity(nc, ident_bf16[:])
        ones_bf16 = const.tile([P, P], BF16, name="ones_bf16", tag="ones_bf16")
        nc.gpsimd.memset(ones_bf16[:], 1.0)
        neg_half = const.tile([P, 2], F32, name="neg_half", tag="neg_half")
        nc.gpsimd.memset(neg_half[:], -0.5)
        eps_col = const.tile([P, 1], F32, name="eps_col", tag="eps_col")
        nc.gpsimd.memset(eps_col[:], EPS)
        scale_all = const.tile([P, K], F32, name="scale_all", tag="scale_all")
        cell_gains = ps_gain.tile([P, 2, H], BF16, name="cell_gains", tag="cell_gains")
        gain_cols = const.tile([P, 4 * GROUPS], F32, name="gain_cols", tag="gain_cols")
        beta_cols = const.tile([P, GROUPS], F32, name="beta_cols", tag="beta_cols")
        near_zero = const.tile([P, GROUPS], F32, name="near_zero", tag="near_zero")
        divisor = const.tile([P, GROUPS], F32, name="divisor", tag="divisor")
        inverse = const.tile([P, GROUPS], F32, name="inverse", tag="inverse")
        ratio_cols = const.tile([P, GROUPS], F32, name="ratio_cols", tag="ratio_cols")
        ratio_all = const.tile([P, 4, BANK], F32, name="ratio_all", tag="ratio_all")

        w_codes = []
        w_scales = []
        for m in range(2):
            codes = const.tile([P, GATES], U32, name="w_codes%d" % m, tag="w_codes%d" % m, align_bytes=64)
            scales = const.tile([P, GATES], U8, name="w_scales%d" % m, tag="w_scales%d" % m, align_bytes=64)
            w_codes.append(codes)
            w_scales.append(scales)
        w_grouped = {}

        def w_interleave(m, q, copy):
            t = stage.tile([P, BANK, PACK], BF16, name="w_grouped_%d_%d" % (m, q), offset=(8 + q) * CHUNK_BYTES)
            copy(
                out=t[:].rearrange("p (c i) j -> p c j i", i=4),
                in_=w_raw[(m, q)].rearrange("p j (c i) -> p c j i", i=4),
            )
            w_grouped[(m, q)] = t

        def w_quantize(m, q):
            cols = slice(q * BANK, (q + 1) * BANK)
            nc.vector.quantize_mx(
                out=w_codes[m][:, cols].bitcast(FP8X4),
                scales=w_scales[m][:, cols],
                in_=w_grouped[(m, q)][:].rearrange("p w j -> p (w j)"),
            )

        x_bf16 = {}
        operand = {}

        def a_widen(n):
            t = prep.tile([P, K], BF16, name="x_bf16", tag="x_bf16", bufs=3)
            nc.vector.tensor_tensor(out=t[:], in0=x_sb[:, n, :].bitcast(FP8), in1=scale_all[:], op=ALU.mult)
            x_bf16[n] = t

        def a_turn(bank, place, n, m):
            words = (h_sb[:, n, :] if m == 0 else x_bf16[n][:]).bitcast(F32)
            for u in range(2):
                nc.tensor.transpose(bank[:, 2 * place + u, :], words[:, u:K // 2:2], ident[:])

        def turn_bank():
            t = ps_back.tile([P, 2 * 2, P], F32, name="back", tag="back")
            return t

        def a_copy(bank, copy):
            t = prep.tile([P, 2 * P * PACK], BF16, name="a_grouped", tag="a_grouped", align_bytes=64)
            copy(
                out=t[:].bitcast(F32).rearrange("p (o r u) -> p o r u", o=2, u=2),
                in_=bank[:].rearrange("p (o u) r -> p o r u", u=2),
            )
            return t

        def a_quantize(grouped, places):
            codes = prep.tile([P, 2 * P], U32, name="a_codes", tag="a_codes", bufs=8, align_bytes=64)
            scales = prep.tile([P, 2 * P], U8, name="a_scales", tag="a_scales", bufs=8, align_bytes=64)
            nc.vector.quantize_mx(out=codes[:].bitcast(FP8X4), scales=scales[:], in_=grouped[:])
            for place, key in enumerate(places):
                cols = slice(place * P, (place + 1) * P)
                operand[key] = (codes[:, cols], scales[:, cols])

        def product_piece(pool, tag, n, m, q):
            cols = slice(q * BANK, (q + 1) * BANK)
            codes, scales = operand[(n, m)]
            acc = pool.tile([P, BANK], F32, name=tag, tag=tag)
            nc.tensor.matmul_mx(
                out=acc[:],
                lhsT=codes.bitcast(FP8X4),
                lhsT_scale=scales,
                rhs=w_codes[m][:, cols].bitcast(FP8X4),
                rhs_scale=w_scales[m][:, cols],
                start=True,
                stop=True,
            )
            return acc

        head = {}
        h_bank = turn_bank()
        a_turn(h_bank, 0, 0, 0)
        a_turn(h_bank, 1, 1, 0)
        scale_ps = ps_unit.tile([P, PACK, P], F32, name="unit_ps", tag="unit_ps")
        for j in range(PACK):
            nc.tensor.transpose(scale_ps[:, j, :], scale_cols[:, j:j + 1].to_broadcast([P, P]), ident[:])
        head["h"] = a_copy(h_bank, nc.scalar.copy)
        nc.scalar.copy(out=scale_all[:].rearrange("p (q j) -> p q j", j=PACK), in_=scale_ps[:].rearrange("p j q -> p q j"))
        w_interleave(0, 0, nc.vector.tensor_copy)
        a_quantize(head["h"], ((0, 0), (1, 0)))
        w_quantize(0, 0)
        w_interleave(0, 1, nc.vector.tensor_copy)

        stat_acc = {}
        norm_acc = {}
        stats = {}
        moments = {}
        factors = {}
        y = {}
        y_count = [0, 0, 0, 0]
        unit_ps = {}
        gate = {}
        spread_ps = {}
        back_ps = {}
        turned = {}
        grouped = {}
        f_c = {}
        c_new = {}
        c_small = {}
        c_normed = {}

        def stat_piece(e):
            pair, w = divmod(e, 16)
            m, v = divmod(w, 8)
            q, r = divmod(v, 2)
            return pair, m, q, r

        def norm_piece(i):
            pair, w = divmod(i, 16)
            m, v = divmod(w, 8)
            g, r = divmod(v, 2)
            return pair, m, g, r

        def unit_place(u):
            pair, w = divmod(u, GROUPS)
            g, jj = divmod(w, 4)
            return pair, g, jj, 4 * GATE_ORDER[g] + jj

        def half_gate(pair, g, half):
            return gate[(pair, g)][:, 2 * half:2 * half + 2, :].rearrange("p j t -> p (j t)")

        def y_tile(g):
            k = y_count[g]
            y_count[g] = k + 1
            tl = stage.tile([P, BANK], F32, name="y_%d_%d" % (g, k), offset=(sum(Y_RING[:g]) + k % Y_RING[g]) * BANK * 4)
            return tl

        def ratio_on_vector(pair, g, r):
            return g > 1 and pair == PAIRS - 1

        def norm_on_vector(pair, m, g, r):
            return pair == PAIRS - 1 and m == 1 and r == 1

        norm_at = {}
        for i in range(PIECES):
            norm_at.setdefault(norm_slot(i), []).append(i)
        unit_at = {}
        for u in range(UNITS):
            unit_at.setdefault(unit_slot(u), []).append(u)
        ratio_at = {}
        for pair in range(PAIRS):
            for k in range(8):
                ratio_at.setdefault(ratio_slot(pair, k), []).append((pair, k // 2, k % 2))
        ig_at = {}
        for pair in range(PAIRS):
            for half in range(2):
                ig_at.setdefault(ig_slot(pair, half), []).append((pair, half))

        def vector_slot(t):
            e = t - 1
            if 0 <= e < PIECES:
                pair, m, q, r = stat_piece(e)
                if e % 8 == 0:
                    tl = small.tile([P, 2, 4, STATS_DIM], F32, name="stats", tag="stats")
                    stats[(pair, m)] = tl
                nc.vector.bn_stats(out=stats[(pair, m)][:, r, q, :], in_=stat_acc[e][:])
            for i in norm_at.get(t - 1, ()):
                pair, m, g, r = norm_piece(i)
                if m == 0 and ratio_on_vector(pair, g, r):
                    tl = y_tile(g)
                    nc.vector.scalar_tensor_tensor(
                        out=tl[:], in0=norm_acc[i][:], scalar=moments[(pair, m)][:, 2 * r:2 * r + 1], in1=ratio_all[:, g, :],
                        op0=ALU.subtract, op1=ALU.mult,
                    )
                    y[(pair, g, r, m)] = tl
                elif norm_on_vector(pair, m, g, r):
                    fac = factors[(pair, m)]
                    tl = y_tile(g)
                    nc.vector.tensor_scalar(
                        out=tl[:], in0=norm_acc[i][:], scalar1=fac[:, r:r + 1], scalar2=fac[:, 2 + r:3 + r], op0=ALU.mult, op1=ALU.add
                    )
                    y[(pair, g, r, m)] = tl
            e = t - 1
            if 0 <= e < PIECES and e % 8 == 7:
                k = stat_piece(e)[0:2]
                mv = small.tile([P, 8], F32, name="moments", tag="moments", bufs=4)
                for r in range(2):
                    nc.vector.bn_aggr(out=mv[:, 2 * r:2 * r + 2], in_=stats[k][:, r, :, :].rearrange("p q s -> p (q s)"))
                fac = small.tile([P, 4], F32, name="factors", tag="factors", bufs=4)
                moments[k] = mv
                factors[k] = fac
            for n in sorted(range(TILES), key=lambda i: (-cell_start(i), i)):
                rows = slice(n * P, (n + 1) * P)
                if t == cell_slot(n, F_C):
                    tl = cell.tile([P, H], F32, name="f_c", tag="f_c", bufs=2)
                    nc.vector.tensor_tensor(out=tl[:], in0=back_ps[("f", n)][:], in1=c_sb[:, n, :], op=ALU.mult)
                    f_c[n] = tl
                elif t == cell_slot(n, C_SUM):
                    tl = cell.tile([P, H], F32, name="c_new", tag="c_new")
                    sm = small.tile([P, 8], F32, name="c_small", tag="c_small", bufs=4)
                    nc.vector.scalar_tensor_tensor(
                        out=tl[:], in0=back_ps[("ig", n)][:], scalar=1.0, in1=f_c[n][:], op0=ALU.mult, op1=ALU.add, accum_out=sm[:, 0:1]
                    )
                    nc.sync.dma_start(out=out_1[rows, :], in_=tl[:])
                    c_new[n] = tl
                    c_small[n] = sm
                elif t == cell_slot(n, C_SUM) + 1:
                    nc.vector.tensor_scalar(out=c_small[n][:, 1:2], in0=c_small[n][:, 0:1], scalar1=-1.0 / H, scalar2=0.0, op0=ALU.mult, op1=ALU.add)
                if t == cell_slot(n, C_SQUARE) + (2 if n < TILES - 4 else 1):
                    sm = c_small[n]
                    nc.vector.tensor_scalar(out=sm[:, 3:4], in0=sm[:, 2:3], scalar1=1.0 / H, scalar2=EPS, op0=ALU.mult, op1=ALU.add)
                    nc.gpsimd.tensor_tensor(out=sm[:, 4:5], in0=sm[:, 3:4], in1=neg_half[:, 0:1], op=ALU.pow)
                if t == cell_slot(n, C_GAIN):
                    tl = cell.tile([P, H], F32, name="c_normed", tag="c_normed")
                    nc.vector.scalar_tensor_tensor(
                        out=tl[:], in0=c_new[n][:], scalar=c_small[n][:, 1:2], in1=cell_gains[:, 0, :], op0=ALU.add, op1=ALU.mult
                    )
                    c_normed[n] = tl
                elif t == cell_slot(n, C_SHIFT):
                    v = c_normed[n][:]
                    nc.vector.scalar_tensor_tensor(
                        out=v, in0=v, scalar=c_small[n][:, 4:5], in1=cell_gains[:, 1, :], op0=ALU.mult, op1=ALU.add
                    )
                elif t == cell_slot(n, H_OUT):
                    tl = cell.tile([P, H], F32, name="h_new", tag="h_new")
                    nc.vector.tensor_tensor(out=tl[:], in0=back_ps[("o", n)][:], in1=c_normed[n][:], op=ALU.mult)
                    nc.sync.dma_start(out=out_0[rows, :], in_=tl[:])
            e = t - 2
            if 0 <= e < PIECES and e % 8 == 7:
                k = stat_piece(e)[0:2]
                nc.gpsimd.tensor_tensor(out=factors[k][:, 0:2], in0=moments[k][:, 4:6], in1=neg_half[:], op=ALU.pow)
                nc.gpsimd.tensor_tensor(out=factors[k][:, 2:4], in0=moments[k][:, 6:8], in1=factors[k][:, 0:2], op=ALU.mult)
            for pair, g, r in ratio_at.get(t, ()):
                if not ratio_on_vector(pair, g, r):
                    v = y[(pair, g, r, 0)][:]
                    nc.gpsimd.tensor_tensor(out=v, in0=v, in1=ratio_all[:, g, :], op=ALU.mult)
            for pair, half in ig_at.get(t, ()):
                iv = half_gate(pair, I_GATE, half)
                nc.gpsimd.tensor_tensor(out=iv, in0=iv, in1=half_gate(pair, G_GATE, half), op=ALU.mult)
            for what, m, q in HEAD_VECTOR.get(t, ()):
                if what == "interleave":
                    w_interleave(m, q, nc.vector.tensor_copy)
                elif what == "quantize":
                    w_quantize(m, q)
                elif what == "widen":
                    a_widen(q)
                else:
                    a_quantize(head["x"], ((0, 1), (1, 1)))
            period, place = divmod(t - CELL_LAG % 8, 8)
            if place == PREP_WIDEN and 3 <= period + 3 < TILES:
                a_widen(period + 3)
            if place == PREP_COPY and 2 <= period + 2 < TILES:
                grouped[period + 2] = a_copy(turned[period + 2], nc.vector.tensor_copy)
            if place == PREP_QUANT and 2 <= period + 2 < TILES:
                n = period + 2
                a_quantize(grouped[n], ((n, 0), (n, 1)))

        HEAD_VECTOR = {
            1: (("quantize", 0, 1),),
            2: (("widen", 1, 0), ("widen", 1, 1)),
            3: (("quantize", 0, 2),),
            4: (("widen", 1, 2),),
            5: (("quantize", 0, 3),),
            7: (("x", 0, 0), ("quantize", 1, 0)),
            9: (("quantize", 1, 1),),
            11: (("quantize", 1, 2),),
            13: (("quantize", 1, 3),),
        }
        HEAD_SCALAR = {
            1: (("interleave", 0, 2), ("interleave", 0, 3)),
            4: (("x", 0, 0), ("interleave", 1, 0)),
            6: (("interleave", 1, 1),),
            8: (("interleave", 1, 2),),
            10: (("interleave", 1, 3),),
        }
        HEAD_TENSOR = {3: "x"}

        def finish_gate(t):
            for u in unit_at.get(t - 1, ()):
                pair, g, jj, j = unit_place(u)
                if jj == 0:
                    tl = gates.tile([P, 4, 2 * P], F32, name="gate%d" % g, tag="gate%d" % g)
                    gate[(pair, g)] = tl
                nc.scalar.activation(
                    out=gate[(pair, g)][:, jj, :],
                    in_=unit_ps[u][:].rearrange("p r t -> p (r t)"),
                    func=(ACT.Tanh if g == G_GATE else ACT.Sigmoid),
                    bias=beta_cols[:, j:j + 1],
                    scale=divisor[:, j:j + 1],
                )

        def normalise(t):
            for i in norm_at.get(t - 2, ()):
                pair, m, g, r = norm_piece(i)
                if m == 0 and ratio_on_vector(pair, g, r):
                    v = y[(pair, g, r, m)][:]
                    nc.scalar.activation(out=v, in_=v, func=ACT.Copy, scale=factors[(pair, m)][:, r:r + 1])
            for i in norm_at.get(t - 1, ()):
                pair, m, g, r = norm_piece(i)
                if not (m == 0 and ratio_on_vector(pair, g, r)) and not norm_on_vector(pair, m, g, r):
                    fac = factors[(pair, m)]
                    tl = y_tile(g)
                    nc.scalar.activation(
                        out=tl[:], in_=norm_acc[i][:], func=ACT.Identity, bias=fac[:, 2 + r:3 + r], scale=fac[:, r:r + 1]
                    )
                    y[(pair, g, r, m)] = tl

        def scalar_slot(t):
            if t % 2 in (0,):
                normalise(t)
                finish_gate(t)
            else:
                finish_gate(t)
                normalise(t)
            for n in range(TILES):
                if t == cell_slot(n, C_SQUARE):
                    sm = c_small[n]
                    sq = cell.tile([P, H], F32, name="square", tag="square", bufs=2)
                    nc.scalar.activation(out=sq[:], in_=c_new[n][:], func=ACT.Square, bias=sm[:, 1:2], accum_out=sm[:, 2:3])
                if t == cell_slot(n, C_TANH):
                    nc.scalar.activation(out=c_normed[n][:], in_=c_normed[n][:], func=ACT.Tanh)
            e = t - 1
            if 0 <= e < PIECES and e % 8 == 7:
                k = stat_piece(e)[0:2]
                nc.scalar.activation(out=moments[k][:, 4:6], in_=moments[k][:, 1:4:2], func=ACT.Identity, bias=eps_col[:])
                nc.scalar.activation(out=moments[k][:, 6:8], in_=moments[k][:, 0:4:2], func=ACT.Identity, scale=-1.0)
            for what, m, q in HEAD_SCALAR.get(t, ()):
                if what == "interleave":
                    w_interleave(m, q, nc.scalar.copy)
                else:
                    head["x"] = a_copy(turned["x"], nc.scalar.copy)
            period, place = divmod(t - CELL_LAG % 8, 8)
            if t == GAIN_COPY_SLOT:
                nc.scalar.copy(out=gain_cols[:], in_=spread_ps["gains"][:, 0:4 * GROUPS])
                nc.gpsimd.tensor_tensor(
                    out=beta_cols[:],
                    in0=gain_cols[:, 2 * GROUPS:3 * GROUPS],
                    in1=gain_cols[:, 3 * GROUPS:4 * GROUPS],
                    op=ALU.add,
                )
                gamma_ih_cols = gain_cols[:, GROUPS:2 * GROUPS]
                nc.gpsimd.tensor_scalar(
                    out=near_zero[:], in0=gamma_ih_cols, scalar1=TINY, scalar2=2.0 * TINY, op0=ALU.is_lt, op1=ALU.mult
                )
                nc.gpsimd.tensor_scalar(
                    out=divisor[:], in0=gamma_ih_cols, scalar1=-TINY, scalar2=1.0, op0=ALU.is_gt, op1=ALU.mult
                )
                nc.gpsimd.tensor_tensor(out=near_zero[:], in0=near_zero[:], in1=divisor[:], op=ALU.mult)
                nc.gpsimd.tensor_tensor(out=divisor[:], in0=gamma_ih_cols, in1=near_zero[:], op=ALU.add)
            if t == GAIN_COPY_SLOT + 4:
                nc.vector.reciprocal(out=inverse[:], in_=divisor[:])
                nc.gpsimd.tensor_tensor(out=ratio_cols[:], in0=gain_cols[:, 0:GROUPS], in1=inverse[:], op=ALU.mult)
            if t - 1 in RATIO_SPREAD_SLOTS:
                g = RATIO_SPREAD_SLOTS.index(t - 1)
                nc.scalar.copy(out=ratio_all[:, g, :], in_=spread_ps[("ratio", g)][:].rearrange("p i c -> p (i c)"))

        def turn_back(what, n, g, half):
            if half == 0:
                if n >= TILES - 2:
                    pool, tag = (ps_stat, "stat_acc") if what == "ig" else (ps_norm, "norm_acc")
                else:
                    pool, tag = ps_back, "back"
                tl = pool.tile([P, H], F32, name=tag, tag=tag)
                back_ps[(what, n)] = tl
            for jj in (2 * half, 2 * half + 1):
                nc.tensor.transpose(
                    back_ps[(what, n)][:, jj * P:(jj + 1) * P],
                    gate[(n // 2, g)][:, jj, (n % 2) * P:(n % 2 + 1) * P],
                    ident[:],
                )

        def turn_slot(t):
            if t == GAIN_TURN_SLOT:
                tl = ps_unit.tile([P, P], BF16, name="unit_ps", tag="unit_ps")
                nc.tensor.transpose(tl[:], gain_rows[:], ident_bf16[:])
                spread_ps["gains"] = tl
            elif t in RATIO_SPREAD_SLOTS:
                g = RATIO_SPREAD_SLOTS.index(t)
                tl = ps_unit.tile([P, 4, P], F32, name="unit_ps", tag="unit_ps")
                for jj in range(4):
                    j = 4 * GATE_ORDER[g] + jj
                    nc.tensor.transpose(tl[:, jj, :], ratio_cols[:, j:j + 1].to_broadcast([P, P]), ident[:])
                spread_ps[("ratio", g)] = tl
            elif t in CELL_GAIN_SPREAD_SLOTS:
                which = CELL_GAIN_SPREAD_SLOTS.index(t)
                nc.tensor.matmul(
                    out=cell_gains[:, which, :], lhsT=ones_bf16[:], rhs=cell_gain_row[:, which * H:(which + 1) * H], start=True, stop=True
                )
            if HEAD_TENSOR.get(t) == "x":
                bank = turn_bank()
                a_turn(bank, 0, 0, 1)
                a_turn(bank, 1, 1, 1)
                turned["x"] = bank
            for u in unit_at.get(t, ()):
                pair, g, jj, j = unit_place(u)
                spare = pair == PAIRS - 1 and g != O_GATE and jj % 2 == 1
                pool, tag = (ps_stat, "stat_acc") if spare else (ps_unit, "unit_ps")
                tl = pool.tile([P, 2, P], F32, name=tag, tag=tag)
                for r in range(2):
                    for m in range(2):
                        nc.tensor.matmul(
                            out=tl[:, r, :],
                            lhsT=y[(pair, g, r, m)][:, jj * P:(jj + 1) * P],
                            rhs=ident[:],
                            is_transpose=True,
                            start=(m == 0),
                            stop=(m == 1),
                        )
                unit_ps[u] = tl
            for n in range(TILES):
                for what, g, step in (("f", F_GATE, F_TURN), ("ig", I_GATE, IG_TURN), ("o", O_GATE, O_TURN)):
                    if t == cell_slot(n, step):
                        turn_back(what, n, g, 0)
                        turn_back(what, n, g, 1)
            period, place = divmod(t - CELL_LAG % 8, 8)
            if place == PREP_TURN and 2 <= period + 2 < TILES:
                n = period + 2
                turned[n] = turn_bank()
                for m in range(2):
                    a_turn(turned[n], m, n, m)

        def product_slot(t):
            if t < PIECES:
                pair, m, q, r = stat_piece(t)
                stat_acc[t] = product_piece(ps_stat, "stat_acc", 2 * pair + r, m, q)
            for i in norm_at.get(t, ()):
                pair, m, g, r = norm_piece(i)
                pool, tag = (ps_stat, "stat_acc") if i >= PIECES - 8 and r == 1 else (ps_norm, "norm_acc")
                norm_acc[i] = product_piece(pool, tag, 2 * pair + r, m, GATE_ORDER[g])

        for t in range(LAST_SLOT + 1):
            vector_slot(t)
            scalar_slot(t)
            if t % 2 in (1,):
                product_slot(t)
                turn_slot(t)
            else:
                turn_slot(t)
                product_slot(t)
